import numpy as np
import ml_dtypes


def mxq(x, axis, fmt="e4m3"):
    dtype, down = {"e4m3": (ml_dtypes.float8_e4m3fn, 7), "e5m2": (ml_dtypes.float8_e5m2, 14)}[fmt]
    v = np.moveaxis(np.asarray(x, np.float32).astype(ml_dtypes.bfloat16).astype(np.float64), axis, -1)
    blocks = v.reshape(v.shape[:-1] + (-1, 32))
    amax = np.abs(blocks).max(-1, keepdims=True)
    byte = np.maximum(np.where(amax > 0, np.frexp(amax)[1] - 1 + 127, 0) - down, 1)
    scale = np.exp2(byte - 127.0)
    codes = (blocks / scale).astype(np.float32).astype(dtype).astype(np.float64)
    return np.moveaxis((codes * scale).reshape(v.shape), -1, axis)


WIDE = False


def mx_kscale(k):
    if not WIDE:
        return np.ones(k)
    levels = np.array([10, -10, 5, -5, 0])
    a = np.random.permutation(np.resize(levels, k // 512 * 4)).reshape(k // 512, 4)
    idx = np.arange(k)
    return np.exp2(a[idx // 512, idx % 128 // 32])


BF16 = ml_dtypes.bfloat16


def bf(x):
    return np.asarray(x, np.float32).astype(BF16)


def f64(x):
    return np.asarray(x).astype(np.float64)


B, T, C, N_HEAD, N_KV, HD, WINDOW = 1, 1024, 1024, 8, 2, 128, 512
QPK = N_HEAD // N_KV
TOT = QPK + 2
QKV_OUT = N_KV * TOT * HD


def apply_rope(xh, fc):
    b, t, h, d = xh.shape
    xs = xh.reshape(b, t, h, d // 2, 2)
    f = fc.reshape(1, t, 1, d // 2, 2)
    re = xs[..., 0] * f[..., 0] - xs[..., 1] * f[..., 1]
    im = xs[..., 1] * f[..., 0] + xs[..., 0] * f[..., 1]
    return np.stack([re, im], axis=-1).reshape(b, t, h, d)


def setup_inputs():
    s = mx_kscale(C)
    inv_freq = 1.0 / (10000.0 ** (np.arange(0, HD, 2) / HD))
    ang = np.outer(np.arange(T), inv_freq)
    return {"x": bf(np.random.standard_normal((B, T, C)) * s),
            "freqs_cis": bf(np.stack([np.cos(ang), np.sin(ang)], axis=-1)),
            "W_attn": bf(np.random.standard_normal((C, QKV_OUT)) * 1.5 / np.sqrt(C) / s[:, None])}


def reference(x, freqs_cis, W_attn):
    qkv = mxq(f64(x), 2, "e4m3") @ mxq(f64(W_attn), 0, "e4m3")
    qkv = qkv.reshape(B, T, N_KV, TOT, HD).transpose(0, 2, 3, 1, 4)
    q = qkv[:, :, :QPK].reshape(B, -1, N_HEAD, HD)
    k = qkv[:, :, QPK:QPK + 1].reshape(B, -1, N_KV, HD)
    v = qkv[:, :, QPK + 1:].reshape(B, -1, N_KV, HD)
    fc = f64(freqs_cis)
    return apply_rope(q, fc), apply_rope(k, fc), v

@@ -1,0 +1,258 @@
+from contextlib import ExitStack
+
+import concourse.mybir as mybir
+from concourse.masks import make_identity
+
+BF16 = mybir.dt.bfloat16
+F32 = mybir.dt.float32
+U32 = mybir.dt.uint32
+U8 = mybir.dt.uint8
+FP8X4 = mybir.dt.float8_e4m3fn_x4
+MULT = mybir.AluOpType.mult
+ADD = mybir.AluOpType.add
+
+P = 128
+PACK = 4
+K_PASS = P * PACK
+TOKENS = 1024
+K = 1024
+PASSES = K // K_PASS
+TILES = TOKENS // P
+HD = 128
+HALF = HD // 2
+GROUPS = 2
+QPK = 4
+SLOT_COLS = (QPK + 2) * HD
+N_COLS = QPK * HD
+SETS = 3
+KV_SET = 2
+HALF_TILES = TILES // 2
+
+FLOPS = 2 * TOKENS * K * GROUPS * SLOT_COLS
+
+
+def rotate_pairs(nc, work, acc, table, dest, slots):
+    pairs = slots * HALF
+    acc_pairs = acc.rearrange("p (s f e) -> p s f e", s=slots, e=2)
+    cos = table[:, :, :, 0:1].to_broadcast([P, slots, HALF, 2])
+    sin = table[:, :, :, 1]
+    by_cos = work.tile([P, QPK * HD], F32, tag="by_cos")
+    nc.vector.tensor_tensor(
+        out=by_cos[:, : slots * HD].rearrange("p (s f e) -> p s f e", s=slots, e=2),
+        in0=acc_pairs,
+        in1=cos,
+        op=MULT,
+    )
+    by_sin = work.tile([P, 2, QPK * HALF], F32, tag="by_sin")
+    nc.vector.scalar_tensor_tensor(
+        out=by_sin[:, 0, :pairs].rearrange("p (s f) -> p s f", s=slots),
+        in0=acc_pairs[:, :, :, 1],
+        scalar=-1.0,
+        in1=sin,
+        op0=MULT,
+        op1=MULT,
+    )
+    nc.vector.tensor_tensor(
+        out=by_sin[:, 1, :pairs].rearrange("p (s f) -> p s f", s=slots),
+        in0=acc_pairs[:, :, :, 0],
+        in1=sin,
+        op=MULT,
+    )
+    nc.gpsimd.tensor_tensor(
+        out=dest.rearrange("p s (f e) -> p s f e", e=2),
+        in0=by_cos[:, : slots * HD].rearrange("p (s f e) -> p s f e", s=slots, e=2),
+        in1=by_sin[:, :, :pairs].rearrange("p e (s f) -> p s f e", s=slots),
+        op=ADD,
+    )
+
+
+def tile_causalselfattentiongqa_pa_kernel(tc, x, freqs_cis, W_attn, out_0, out_1, out_2):
+    nc = tc.nc
+    with ExitStack() as ctx:
+        keep = ctx.enter_context(tc.tile_pool(name="keep", bufs=1))
+        work = ctx.enter_context(tc.tile_pool(name="work", bufs=3))
+        stage = ctx.enter_context(tc.tile_pool(name="stage", bufs=4))
+        psum_t = ctx.enter_context(tc.psum_pool(name="psum_t", bufs=2))
+        psum_acc = ctx.enter_context(tc.psum_pool(name="psum_acc", bufs=6))
+
+        x_view = x.flatten_outer_dims().rearrange("(i j) k -> i (j k)", j=TILES)
+        w_view = W_attn.rearrange("(c p t) n -> p c t n", c=PASSES, t=PACK)
+        q_view = out_0.rearrange("o n h d -> (o n h) d").rearrange(
+            "(a i j) d -> i a j d", a=GROUPS * QPK, j=TILES
+        )
+        k_view = out_1.rearrange("o n h d -> (o n h) d").rearrange(
+            "(g i j) d -> i g j d", g=GROUPS, j=TILES
+        )
+        v_view = out_2.rearrange("o n h d -> (o n h) d").rearrange(
+            "(g i j) d -> i g j d", g=GROUPS, j=TILES
+        )
+
+        x_sb = keep.tile([P, TILES * K], BF16)
+        x_grouped = keep.tile([P, TILES * K], BF16, align_bytes=64)
+        x_codes = keep.tile([P, TILES * PASSES * P], U32, align_bytes=64)
+        x_scales = keep.tile([P, TILES * PASSES * P], U8, align_bytes=64)
+        w_raw = keep.tile([P, SETS, PASSES, PACK, N_COLS], BF16)
+        w_grouped = keep.tile([P, SETS, PASSES, N_COLS, PACK], BF16, align_bytes=64)
+        w_codes = keep.tile([P, SETS, PASSES, N_COLS], U32, align_bytes=64)
+        w_scales = keep.tile([P, SETS, PASSES, N_COLS], U8, align_bytes=64)
+        q_table = keep.tile([P, GROUPS * QPK, HALF, 2], BF16)
+        k_table = keep.tile([P, GROUPS, TILES // 2, HALF, 2], BF16)
+        identity = keep.tile([P, P], F32)
+        k_stage = keep.tile([P, GROUPS, TILES, HD], F32)
+        v_stage = keep.tile([P, GROUPS, TILES, HD], F32)
+
+        make_identity(nc, identity[:])
+
+        def load_x(pair):
+            cols = slice(pair * 2 * K, (pair + 1) * 2 * K)
+            nc.sync.dma_start(out=x_sb[:, cols], in_=x_view[:, cols])
+
+        def load_w(s, c, first_col, width, at):
+            nc.sync.dma_start(
+                out=w_raw[:, s, c, :, at : at + width],
+                in_=w_view[:, c, :, first_col : first_col + width],
+            )
+
+        for c in range(PASSES):
+            load_w(0, c, 0, N_COLS, 0)
+        load_x(0)
+        nc.sync.dma_start(
+            out=q_table[:], in_=freqs_cis.rearrange("(a i) f e -> i a f e", a=GROUPS * QPK)
+        )
+        for pair in range(1, TILES // 2):
+            load_x(pair)
+        for c in range(PASSES):
+            load_w(1, c, SLOT_COLS, N_COLS, 0)
+        nc.sync.dma_start(
+            out=k_table[:],
+            in_=freqs_cis.rearrange("(g i r) f e -> i g r f e", g=GROUPS, r=TILES // 2),
+        )
+        for c in range(PASSES):
+            for g in range(GROUPS):
+                load_w(KV_SET, c, g * SLOT_COLS + N_COLS, 2 * HD, g * 2 * HD)
+
+        def regroup_w(copy, s, c):
+            copy(
+                out=w_grouped[:, s, c, :, :].rearrange("p (n i) t -> p n t i", i=4),
+                in_=w_raw[:, s, c, :, :].rearrange("p t (n i) -> p n t i", i=4),
+            )
+
+        def quantise_w(s, c):
+            nc.vector.quantize_mx(
+                out=w_codes[:, s, c, :].bitcast(FP8X4),
+                scales=w_scales[:, s, c, :],
+                in_=w_grouped[:, s, c, :, :].rearrange("p n t -> p (n t)"),
+            )
+
+        x_words = x_sb[:].bitcast(F32).rearrange(
+            "i (j c p u) -> i j c u p", j=TILES, c=PASSES, u=2
+        )
+
+        def prepare_x(j):
+            turned = psum_t.tile([P, PASSES * 2, P], F32, tag="turned")
+            for c in range(PASSES):
+                for u in range(2):
+                    nc.tensor.transpose(turned[:, 2 * c + u, :], x_words[:, j, c, u, :], identity[:])
+            cols = slice(j * K, (j + 1) * K)
+            nc.scalar.copy(
+                out=x_grouped[:, cols].bitcast(F32).rearrange("p (c i u) -> p c i u", c=PASSES, u=2),
+                in_=turned[:].rearrange("p (c u) i -> p c i u", c=PASSES),
+            )
+
+        def quantise_x(j):
+            words = slice(j * PASSES * P, (j + 1) * PASSES * P)
+            nc.vector.quantize_mx(
+                out=x_codes[:, words].bitcast(FP8X4),
+                scales=x_scales[:, words],
+                in_=x_grouped[:, j * K : (j + 1) * K],
+            )
+
+        def project(acc, j, s, first_col, width):
+            for c in range(PASSES):
+                tokens = slice((j * PASSES + c) * P, (j * PASSES + c + 1) * P)
+                nc.tensor.matmul_mx(
+                    out=acc,
+                    lhsT=x_codes[:, tokens].bitcast(FP8X4),
+                    lhsT_scale=x_scales[:, tokens],
+                    rhs=w_codes[:, s, c, first_col : first_col + width].bitcast(FP8X4),
+                    rhs_scale=w_scales[:, s, c, first_col : first_col + width],
+                    start=(c == 0),
+                    stop=(c == PASSES - 1),
+                )
+
+        def queries(s, j, q_stage):
+            acc = psum_acc.tile([P, N_COLS], F32, tag="acc")
+            project(acc[:], j, s, 0, N_COLS)
+            rotate_pairs(
+                nc,
+                work,
+                acc[:],
+                q_table[:, s * QPK : (s + 1) * QPK, :, :],
+                q_stage[:, :, j % HALF_TILES, :],
+                QPK,
+            )
+
+        def store_queries(s, half, q_stage):
+            nc.sync.dma_start(
+                out=q_view[
+                    :, s * QPK : (s + 1) * QPK, half * HALF_TILES : (half + 1) * HALF_TILES, :
+                ],
+                in_=q_stage[:],
+            )
+
+        for c in range(PASSES):
+            regroup_w(nc.vector.tensor_copy, 0, c)
+        for c in range(PASSES):
+            quantise_w(0, c)
+        for j in range(2):
+            prepare_x(j)
+        for j in range(2):
+            quantise_x(j)
+        for half in range(2):
+            q_stage = stage.tile([P, QPK, HALF_TILES, HD], F32, tag="q_stage")
+            for pair in range(2 * half, 2 * half + 2):
+                if pair + 1 < TILES // 2:
+                    for j in range(2 * pair + 2, 2 * pair + 4):
+                        prepare_x(j)
+                    for j in range(2 * pair + 2, 2 * pair + 4):
+                        quantise_x(j)
+                for j in range(2 * pair, 2 * pair + 2):
+                    queries(0, j, q_stage)
+            store_queries(0, half, q_stage)
+
+        for s in range(1, SETS):
+            for c in range(PASSES):
+                regroup_w(nc.scalar.copy, s, c)
+        for c in range(PASSES):
+            quantise_w(1, c)
+        for half in range(2):
+            q_stage = stage.tile([P, QPK, HALF_TILES, HD], F32, tag="q_stage")
+            for j in range(half * HALF_TILES, (half + 1) * HALF_TILES):
+                queries(1, j, q_stage)
+            store_queries(1, half, q_stage)
+
+        for c in range(PASSES):
+            quantise_w(KV_SET, c)
+        for j in range(TILES):
+            k_acc = psum_acc.tile([P, N_COLS], F32, tag="acc")
+            v_acc = psum_acc.tile([P, N_COLS], F32, tag="acc")
+            for g in range(GROUPS):
+                project(k_acc[:, g * HD : (g + 1) * HD], j, KV_SET, g * 2 * HD, HD)
+            for g in range(GROUPS):
+                project(v_acc[:, g * HD : (g + 1) * HD], j, KV_SET, g * 2 * HD + HD, HD)
+            rotate_pairs(
+                nc,
+                work,
+                k_acc[:, : GROUPS * HD],
+                k_table[:, :, j // 2, :, :],
+                k_stage[:, :, j, :],
+                GROUPS,
+            )
+            nc.scalar.copy(
+                out=v_stage[:, :, j, :],
+                in_=v_acc[:, : GROUPS * HD].rearrange("p (g d) -> p g d", g=GROUPS),
+            )
+            if j % HALF_TILES == HALF_TILES - 1:
+                done = slice(j + 1 - HALF_TILES, j + 1)
+                nc.sync.dma_start(out=k_view[:, :, done, :], in_=k_stage[:, :, done, :])
+                nc.sync.dma_start(out=v_view[:, :, done, :], in_=v_stage[:, :, done, :])

@@ -31,38 +31,37 @@ HALF_TILES = TILES // 2
 FLOPS = 2 * TOKENS * K * GROUPS * SLOT_COLS
 
 
-def rotate_pairs(nc, work, acc, table, dest, slots):
-    pairs = slots * HALF
+def rotate_pairs(nc, work, acc, table, turned_table, dest, slots):
     acc_pairs = acc.rearrange("p (s f e) -> p s f e", s=slots, e=2)
-    cos = table[:, :, :, 0:1].to_broadcast([P, slots, HALF, 2])
-    sin = table[:, :, :, 1]
-    by_cos = work.tile([P, QPK * HD], F32, tag="by_cos")
+    shape = [P, slots, HALF, 2]
+    by_a = work.tile([P, QPK * HD], F32, tag="by_a")
     nc.vector.tensor_tensor(
-        out=by_cos[:, : slots * HD].rearrange("p (s f e) -> p s f e", s=slots, e=2),
-        in0=acc_pairs,
-        in1=cos,
+        out=by_a[:, : slots * HD].rearrange("p (s f e) -> p s f e", s=slots, e=2),
+        in0=acc_pairs[:, :, :, 0:1].to_broadcast(shape),
+        in1=table,
         op=MULT,
     )
-    by_sin = work.tile([P, 2, QPK * HALF], F32, tag="by_sin")
-    nc.vector.scalar_tensor_tensor(
-        out=by_sin[:, 0, :pairs].rearrange("p (s f) -> p s f", s=slots),
-        in0=acc_pairs[:, :, :, 1],
-        scalar=-1.0,
-        in1=sin,
-        op0=MULT,
-        op1=MULT,
-    )
+    by_b = work.tile([P, QPK * HD], F32, tag="by_b")
     nc.vector.tensor_tensor(
-        out=by_sin[:, 1, :pairs].rearrange("p (s f) -> p s f", s=slots),
-        in0=acc_pairs[:, :, :, 0],
-        in1=sin,
+        out=by_b[:, : slots * HD].rearrange("p (s f e) -> p s f e", s=slots, e=2),
+        in0=acc_pairs[:, :, :, 1:2].to_broadcast(shape),
+        in1=turned_table,
         op=MULT,
     )
     nc.gpsimd.tensor_tensor(
-        out=dest.rearrange("p s (f e) -> p s f e", e=2),
-        in0=by_cos[:, : slots * HD].rearrange("p (s f e) -> p s f e", s=slots, e=2),
-        in1=by_sin[:, :, :pairs].rearrange("p e (s f) -> p s f e", s=slots),
+        out=dest,
+        in0=by_a[:, : slots * HD].rearrange("p (s d) -> p s d", s=slots),
+        in1=by_b[:, : slots * HD].rearrange("p (s d) -> p s d", s=slots),
         op=ADD,
+    )
+
+
+def turn_table(nc, turned_table, table):
+    nc.gpsimd.tensor_scalar(
+        out=turned_table[:, :, :, 0], in0=table[:, :, :, 1], scalar1=-1.0, scalar2=0.0, op0=MULT, op1=ADD
+    )
+    nc.gpsimd.tensor_scalar(
+        out=turned_table[:, :, :, 1], in0=table[:, :, :, 0], scalar1=1.0, scalar2=0.0, op0=MULT, op1=ADD
     )
 
 
@@ -97,6 +96,8 @@ def tile_causalselfattentiongqa_pa_kernel(tc, x, freqs_cis, W_attn, out_0, out_1
         w_scales = keep.tile([P, SETS, PASSES, N_COLS], U8, align_bytes=64)
         q_table = keep.tile([P, GROUPS * QPK, HALF, 2], BF16)
         k_table = keep.tile([P, GROUPS, TILES // 2, HALF, 2], BF16)
+        q_turned = keep.tile([P, GROUPS * QPK, HALF, 2], BF16)
+        k_turned = keep.tile([P, GROUPS, TILES // 2, HALF, 2], BF16)
         identity = keep.tile([P, P], F32)
         k_stage = keep.tile([P, GROUPS, TILES, HD], F32)
         v_stage = keep.tile([P, GROUPS, TILES, HD], F32)
@@ -130,6 +131,13 @@ def tile_causalselfattentiongqa_pa_kernel(tc, x, freqs_cis, W_attn, out_0, out_1
         for c in range(PASSES):
             for g in range(GROUPS):
                 load_w(KV_SET, c, g * SLOT_COLS + N_COLS, 2 * HD, g * 2 * HD)
+
+        turn_table(nc, q_turned[:], q_table[:])
+        turn_table(
+            nc,
+            k_turned[:].rearrange("p g r f e -> p (g r) f e"),
+            k_table[:].rearrange("p g r f e -> p (g r) f e"),
+        )
 
         def regroup_w(copy, s, c):
             copy(
@@ -188,6 +196,7 @@ def tile_causalselfattentiongqa_pa_kernel(tc, x, freqs_cis, W_attn, out_0, out_1
                 work,
                 acc[:],
                 q_table[:, s * QPK : (s + 1) * QPK, :, :],
+                q_turned[:, s * QPK : (s + 1) * QPK, :, :],
                 q_stage[:, :, j % HALF_TILES, :],
                 QPK,
             )
@@ -245,6 +254,7 @@ def tile_causalselfattentiongqa_pa_kernel(tc, x, freqs_cis, W_attn, out_0, out_1
                 work,
                 k_acc[:, : GROUPS * HD],
                 k_table[:, :, j // 2, :, :],
+                k_turned[:, :, j // 2, :, :],
                 k_stage[:, :, j, :],
                 GROUPS,
             )

@@ -10,6 +10,7 @@ U8 = mybir.dt.uint8
 FP8X4 = mybir.dt.float8_e4m3fn_x4
 MULT = mybir.AluOpType.mult
 ADD = mybir.AluOpType.add
+COPY = mybir.ActivationFunctionType.Copy
 
 P = 128
 PACK = 4
@@ -22,55 +23,38 @@ HD = 128
 HALF = HD // 2
 GROUPS = 2
 QPK = 4
-SLOT_COLS = (QPK + 2) * HD
-N_COLS = QPK * HD
-SETS = 3
-KV_SET = 2
-HALF_TILES = TILES // 2
+GROUP_SLOTS = QPK + 2
+KEY = QPK
+VALUE = QPK + 1
+BANK_TILES = 4
 
-FLOPS = 2 * TOKENS * K * GROUPS * SLOT_COLS
+FLOPS = 2 * TOKENS * K * GROUPS * GROUP_SLOTS * HD
 
-
-def rotate_pairs(nc, work, acc, table, turned_table, dest, slots):
-    acc_pairs = acc.rearrange("p (s f e) -> p s f e", s=slots, e=2)
-    shape = [P, slots, HALF, 2]
-    by_a = work.tile([P, QPK * HD], F32, tag="by_a")
-    nc.vector.tensor_tensor(
-        out=by_a[:, : slots * HD].rearrange("p (s f e) -> p s f e", s=slots, e=2),
-        in0=acc_pairs[:, :, :, 0:1].to_broadcast(shape),
-        in1=table,
-        op=MULT,
-    )
-    by_b = work.tile([P, QPK * HD], F32, tag="by_b")
-    nc.vector.tensor_tensor(
-        out=by_b[:, : slots * HD].rearrange("p (s f e) -> p s f e", s=slots, e=2),
-        in0=acc_pairs[:, :, :, 1:2].to_broadcast(shape),
-        in1=turned_table,
-        op=MULT,
-    )
-    nc.gpsimd.tensor_tensor(
-        out=dest,
-        in0=by_a[:, : slots * HD].rearrange("p (s d) -> p s d", s=slots),
-        in1=by_b[:, : slots * HD].rearrange("p (s d) -> p s d", s=slots),
-        op=ADD,
-    )
-
-
-def turn_table(nc, turned_table, table):
-    nc.gpsimd.tensor_scalar(
-        out=turned_table[:, :, :, 0], in0=table[:, :, :, 1], scalar1=-1.0, scalar2=0.0, op0=MULT, op1=ADD
-    )
-    nc.gpsimd.tensor_scalar(
-        out=turned_table[:, :, :, 1], in0=table[:, :, :, 0], scalar1=1.0, scalar2=0.0, op0=MULT, op1=ADD
-    )
+CHUNKS = ((0, 2), (2, 2), (4, 2), (6, 4), (10, 2))
+X_LOADS = ((0,), (1,), (2, 3), (4, 5), (6, 7))
+X_QUANTS = ((0,), (1,), (2, 3), (4, 5, 6, 7))
+HEAD_UNITS = ((0, 0, 1), (0, 1, 1), (1, 0, 2), (0, 2, 2), (1, 2, 2), (2, 0, 4), (3, 0, 4))
+HEAD_REST = ((0, 4, 4), (1, 4, 4), (2, 4, 4), (3, 4, 4))
+LATER_SLOTS = (5, 4, 6, 7, 8, 9, 11, 10)
+LEAD_REGROUP = 5
+LEAD_QUANTISE = 4
+LEAD_MULTIPLY = 2
 
 
 def tile_causalselfattentiongqa_pa_kernel(tc, x, freqs_cis, W_attn, out_0, out_1, out_2):
     nc = tc.nc
+    units = list(HEAD_UNITS) + list(HEAD_REST)
+    for slot in LATER_SLOTS:
+        for first in range(0, TILES, BANK_TILES):
+            units.append((slot, first, BANK_TILES))
+    chunk_of = {}
+    for ch, (first_slot, slots) in enumerate(CHUNKS):
+        for slot in range(first_slot, first_slot + slots):
+            chunk_of[slot] = ch
+
     with ExitStack() as ctx:
         keep = ctx.enter_context(tc.tile_pool(name="keep", bufs=1))
-        work = ctx.enter_context(tc.tile_pool(name="work", bufs=3))
-        stage = ctx.enter_context(tc.tile_pool(name="stage", bufs=4))
+        work = ctx.enter_context(tc.tile_pool(name="work", bufs=6))
         psum_t = ctx.enter_context(tc.psum_pool(name="psum_t", bufs=2))
         psum_acc = ctx.enter_context(tc.psum_pool(name="psum_acc", bufs=6))
 
@@ -85,78 +69,87 @@ def tile_causalselfattentiongqa_pa_kernel(tc, x, freqs_cis, W_attn, out_0, out_1
         v_view = out_2.rearrange("o n h d -> (o n h) d").rearrange(
             "(g i j) d -> i g j d", g=GROUPS, j=TILES
         )
+        q_freqs = freqs_cis.rearrange("(a i) f e -> i a f e", a=GROUPS * QPK)
+        k_freqs = freqs_cis.rearrange("(g i r) f e -> i g r f e", g=GROUPS, r=TILES // 2)
 
         x_sb = keep.tile([P, TILES * K], BF16)
         x_grouped = keep.tile([P, TILES * K], BF16, align_bytes=64)
         x_codes = keep.tile([P, TILES * PASSES * P], U32, align_bytes=64)
         x_scales = keep.tile([P, TILES * PASSES * P], U8, align_bytes=64)
-        w_raw = keep.tile([P, SETS, PASSES, PACK, N_COLS], BF16)
-        w_grouped = keep.tile([P, SETS, PASSES, N_COLS, PACK], BF16, align_bytes=64)
-        w_codes = keep.tile([P, SETS, PASSES, N_COLS], U32, align_bytes=64)
-        w_scales = keep.tile([P, SETS, PASSES, N_COLS], U8, align_bytes=64)
-        q_table = keep.tile([P, GROUPS * QPK, HALF, 2], BF16)
-        k_table = keep.tile([P, GROUPS, TILES // 2, HALF, 2], BF16)
-        q_turned = keep.tile([P, GROUPS * QPK, HALF, 2], BF16)
-        k_turned = keep.tile([P, GROUPS, TILES // 2, HALF, 2], BF16)
+        w_raw = []
+        w_grouped = []
+        w_codes = []
+        w_scales = []
+        for ch, (first_slot, slots) in enumerate(CHUNKS):
+            cols = slots * HD
+            w_raw.append(keep.tile([P, PASSES, PACK, cols], BF16, name="w_raw%d" % ch))
+            w_grouped.append(
+                keep.tile([P, PASSES, cols, PACK], BF16, name="w_grouped%d" % ch, align_bytes=64)
+            )
+            w_codes.append(keep.tile([P, PASSES, cols], U32, name="w_codes%d" % ch, align_bytes=64))
+            w_scales.append(keep.tile([P, PASSES, cols], U8, name="w_scales%d" % ch, align_bytes=64))
+        q_table = keep.tile([P, GROUPS * QPK, 2, HALF, 2], BF16)
+        k_table = keep.tile([P, GROUPS * TILES // 2, 2, HALF, 2], BF16)
         identity = keep.tile([P, P], F32)
-        k_stage = keep.tile([P, GROUPS, TILES, HD], F32)
-        v_stage = keep.tile([P, GROUPS, TILES, HD], F32)
 
         make_identity(nc, identity[:])
 
-        def load_x(pair):
-            cols = slice(pair * 2 * K, (pair + 1) * 2 * K)
+        def load_x(tiles):
+            cols = slice(tiles[0] * K, (tiles[-1] + 1) * K)
             nc.sync.dma_start(out=x_sb[:, cols], in_=x_view[:, cols])
 
-        def load_w(s, c, first_col, width, at):
-            nc.sync.dma_start(
-                out=w_raw[:, s, c, :, at : at + width],
-                in_=w_view[:, c, :, first_col : first_col + width],
-            )
+        def load_w(ch):
+            first_slot, slots = CHUNKS[ch]
+            for c in range(PASSES):
+                nc.sync.dma_start(
+                    out=w_raw[ch][:, c, :, :],
+                    in_=w_view[:, c, :, first_slot * HD : (first_slot + slots) * HD],
+                )
 
-        for c in range(PASSES):
-            load_w(0, c, 0, N_COLS, 0)
-        load_x(0)
-        nc.sync.dma_start(
-            out=q_table[:], in_=freqs_cis.rearrange("(a i) f e -> i a f e", a=GROUPS * QPK)
-        )
-        for pair in range(1, TILES // 2):
-            load_x(pair)
-        for c in range(PASSES):
-            load_w(1, c, SLOT_COLS, N_COLS, 0)
-        nc.sync.dma_start(
-            out=k_table[:],
-            in_=freqs_cis.rearrange("(g i r) f e -> i g r f e", g=GROUPS, r=TILES // 2),
-        )
-        for c in range(PASSES):
-            for g in range(GROUPS):
-                load_w(KV_SET, c, g * SLOT_COLS + N_COLS, 2 * HD, g * 2 * HD)
+        def load_q_table(g):
+            rows = slice(g * QPK, (g + 1) * QPK)
+            nc.sync.dma_start(out=q_table[:, rows, 0, :, :], in_=q_freqs[:, rows, :, :])
 
-        turn_table(nc, q_turned[:], q_table[:])
-        turn_table(
-            nc,
-            k_turned[:].rearrange("p g r f e -> p (g r) f e"),
-            k_table[:].rearrange("p g r f e -> p (g r) f e"),
-        )
+        load_q_table(0)
+        load_x(X_LOADS[0])
+        load_w(0)
+        load_x(X_LOADS[1])
+        load_x(X_LOADS[2])
+        load_w(1)
+        load_x(X_LOADS[3])
+        load_x(X_LOADS[4])
+        load_w(2)
+        for g in range(GROUPS):
+            rows = slice(g * (TILES // 2), (g + 1) * (TILES // 2))
+            nc.sync.dma_start(out=k_table[:, rows, 0, :, :], in_=k_freqs[:, g, :, :, :])
+        load_q_table(1)
+        load_w(3)
+        load_w(4)
 
-        def regroup_w(copy, s, c):
-            copy(
-                out=w_grouped[:, s, c, :, :].rearrange("p (n i) t -> p n t i", i=4),
-                in_=w_raw[:, s, c, :, :].rearrange("p t (n i) -> p n t i", i=4),
-            )
+        def turn_table(table):
+            nc.scalar.activation(out=table[:, :, 1, :, 0], in_=table[:, :, 0, :, 1], func=COPY, scale=-1.0)
+            nc.scalar.copy(out=table[:, :, 1, :, 1], in_=table[:, :, 0, :, 0])
 
-        def quantise_w(s, c):
+        def regroup_w(ch):
+            copy = nc.vector.tensor_copy if ch == 0 else nc.scalar.copy
+            for c in range(PASSES):
+                copy(
+                    out=w_grouped[ch][:, c, :, :].rearrange("p (n i) t -> p n t i", i=4),
+                    in_=w_raw[ch][:, c, :, :].rearrange("p t (n i) -> p n t i", i=4),
+                )
+
+        def quantise_w(ch):
             nc.vector.quantize_mx(
-                out=w_codes[:, s, c, :].bitcast(FP8X4),
-                scales=w_scales[:, s, c, :],
-                in_=w_grouped[:, s, c, :, :].rearrange("p n t -> p (n t)"),
+                out=w_codes[ch][:].rearrange("p c n -> p (c n)").bitcast(FP8X4),
+                scales=w_scales[ch][:].rearrange("p c n -> p (c n)"),
+                in_=w_grouped[ch][:].rearrange("p c n t -> p (c n t)"),
             )
 
         x_words = x_sb[:].bitcast(F32).rearrange(
             "i (j c p u) -> i j c u p", j=TILES, c=PASSES, u=2
         )
 
-        def prepare_x(j):
+        def turn_x(j):
             turned = psum_t.tile([P, PASSES * 2, P], F32, tag="turned")
             for c in range(PASSES):
                 for u in range(2):
@@ -167,102 +160,109 @@ def tile_causalselfattentiongqa_pa_kernel(tc, x, freqs_cis, W_attn, out_0, out_1
                 in_=turned[:].rearrange("p (c u) i -> p c i u", c=PASSES),
             )
 
-        def quantise_x(j):
-            words = slice(j * PASSES * P, (j + 1) * PASSES * P)
+        def quantise_x(tiles):
+            first, after = tiles[0], tiles[-1] + 1
+            words = slice(first * PASSES * P, after * PASSES * P)
             nc.vector.quantize_mx(
                 out=x_codes[:, words].bitcast(FP8X4),
                 scales=x_scales[:, words],
-                in_=x_grouped[:, j * K : (j + 1) * K],
+                in_=x_grouped[:, first * K : after * K],
             )
 
-        def project(acc, j, s, first_col, width):
-            for c in range(PASSES):
-                tokens = slice((j * PASSES + c) * P, (j * PASSES + c + 1) * P)
-                nc.tensor.matmul_mx(
-                    out=acc,
-                    lhsT=x_codes[:, tokens].bitcast(FP8X4),
-                    lhsT_scale=x_scales[:, tokens],
-                    rhs=w_codes[:, s, c, first_col : first_col + width].bitcast(FP8X4),
-                    rhs_scale=w_scales[:, s, c, first_col : first_col + width],
-                    start=(c == 0),
-                    stop=(c == PASSES - 1),
-                )
+        def multiply(unit):
+            slot, first, tiles = unit
+            ch = chunk_of[slot]
+            cols = slice((slot - CHUNKS[ch][0]) * HD, (slot - CHUNKS[ch][0] + 1) * HD)
+            acc = psum_acc.tile([P, BANK_TILES * HD], F32, tag="acc")
+            for n in range(tiles):
+                for c in range(PASSES):
+                    tokens = slice(((first + n) * PASSES + c) * P, ((first + n) * PASSES + c + 1) * P)
+                    nc.tensor.matmul_mx(
+                        out=acc[:, n * HD : (n + 1) * HD],
+                        lhsT=x_codes[:, tokens].bitcast(FP8X4),
+                        lhsT_scale=x_scales[:, tokens],
+                        rhs=w_codes[ch][:, c, cols].bitcast(FP8X4),
+                        rhs_scale=w_scales[ch][:, c, cols],
+                        start=(c == 0),
+                        stop=(c == PASSES - 1),
+                    )
+            return acc
 
-        def queries(s, j, q_stage):
-            acc = psum_acc.tile([P, N_COLS], F32, tag="acc")
-            project(acc[:], j, s, 0, N_COLS)
-            rotate_pairs(
-                nc,
-                work,
-                acc[:],
-                q_table[:, s * QPK : (s + 1) * QPK, :, :],
-                q_turned[:, s * QPK : (s + 1) * QPK, :, :],
-                q_stage[:, :, j % HALF_TILES, :],
-                QPK,
+        def products(dest, acc, table, row, first, tiles):
+            shape = [P, 2, tiles, HALF, 2]
+            cols = slice(first * HD, (first + tiles) * HD)
+            nc.vector.tensor_tensor(
+                out=dest[:, :, cols].rearrange("p h (j f e) -> p h j f e", f=HALF, e=2),
+                in0=acc[:, cols]
+                .rearrange("p (j f h) -> p h j f", f=HALF, h=2)
+                .unsqueeze(4)
+                .to_broadcast(shape),
+                in1=table[:, row, :, :, :].unsqueeze(2).to_broadcast(shape),
+                op=MULT,
             )
 
-        def store_queries(s, half, q_stage):
-            nc.sync.dma_start(
-                out=q_view[
-                    :, s * QPK : (s + 1) * QPK, half * HALF_TILES : (half + 1) * HALF_TILES, :
-                ],
-                in_=q_stage[:],
-            )
+        def finish(unit, acc, add):
+            slot, first, tiles = unit
+            g, place = divmod(slot, GROUP_SLOTS)
+            width = tiles * HD
+            rows = work.tile([P, BANK_TILES * HD], F32, tag="rows")
+            if place == VALUE:
+                nc.scalar.copy(out=rows[:, :width], in_=acc[:, :width])
+                dest = v_view[:, g, first : first + tiles, :]
+            else:
+                both = work.tile([P, 2, BANK_TILES * HD], F32, tag="both")
+                if place == KEY:
+                    for n in range(0, tiles, 2):
+                        products(both, acc, k_table, g * (TILES // 2) + (first + n) // 2, n, 2)
+                    dest = k_view[:, g, first : first + tiles, :]
+                else:
+                    products(both, acc, q_table, g * QPK + place, 0, tiles)
+                    dest = q_view[:, g * QPK + place, first : first + tiles, :]
+                add(out=rows[:, :width], in0=both[:, 0, :width], in1=both[:, 1, :width], op=ADD)
+            nc.sync.dma_start(out=dest, in_=rows[:, :width].rearrange("p (j d) -> p j d", d=HD))
 
-        for c in range(PASSES):
-            regroup_w(nc.vector.tensor_copy, 0, c)
-        for c in range(PASSES):
-            quantise_w(0, c)
-        for j in range(2):
-            prepare_x(j)
-        for j in range(2):
-            quantise_x(j)
-        for half in range(2):
-            q_stage = stage.tile([P, QPK, HALF_TILES, HD], F32, tag="q_stage")
-            for pair in range(2 * half, 2 * half + 2):
-                if pair + 1 < TILES // 2:
-                    for j in range(2 * pair + 2, 2 * pair + 4):
-                        prepare_x(j)
-                    for j in range(2 * pair + 2, 2 * pair + 4):
-                        quantise_x(j)
-                for j in range(2 * pair, 2 * pair + 2):
-                    queries(0, j, q_stage)
-            store_queries(0, half, q_stage)
+        turned_x = set()
+        quantised_x = set()
+        regrouped = set()
+        quantised_w = set()
+        tables = set()
+        accs = {}
 
-        for s in range(1, SETS):
-            for c in range(PASSES):
-                regroup_w(nc.scalar.copy, s, c)
-        for c in range(PASSES):
-            quantise_w(1, c)
-        for half in range(2):
-            q_stage = stage.tile([P, QPK, HALF_TILES, HD], F32, tag="q_stage")
-            for j in range(half * HALF_TILES, (half + 1) * HALF_TILES):
-                queries(1, j, q_stage)
-            store_queries(1, half, q_stage)
+        def regroup_for(unit):
+            slot, first, tiles = unit
+            g, place = divmod(slot, GROUP_SLOTS)
+            if place < QPK and ("q", g) not in tables:
+                tables.add(("q", g))
+                rows = slice(g * QPK, (g + 1) * QPK)
+                turn_table(q_table[:, rows, :, :, :])
+            if place == KEY and "k" not in tables:
+                tables.add("k")
+                turn_table(k_table[:])
+            for j in range(first, first + tiles):
+                if j not in turned_x:
+                    turned_x.add(j)
+                    turn_x(j)
+            if chunk_of[slot] not in regrouped:
+                regrouped.add(chunk_of[slot])
+                regroup_w(chunk_of[slot])
 
-        for c in range(PASSES):
-            quantise_w(KV_SET, c)
-        for j in range(TILES):
-            k_acc = psum_acc.tile([P, N_COLS], F32, tag="acc")
-            v_acc = psum_acc.tile([P, N_COLS], F32, tag="acc")
-            for g in range(GROUPS):
-                project(k_acc[:, g * HD : (g + 1) * HD], j, KV_SET, g * 2 * HD, HD)
-            for g in range(GROUPS):
-                project(v_acc[:, g * HD : (g + 1) * HD], j, KV_SET, g * 2 * HD + HD, HD)
-            rotate_pairs(
-                nc,
-                work,
-                k_acc[:, : GROUPS * HD],
-                k_table[:, :, j // 2, :, :],
-                k_turned[:, :, j // 2, :, :],
-                k_stage[:, :, j, :],
-                GROUPS,
-            )
-            nc.scalar.copy(
-                out=v_stage[:, :, j, :],
-                in_=v_acc[:, : GROUPS * HD].rearrange("p (g d) -> p g d", g=GROUPS),
-            )
-            if j % HALF_TILES == HALF_TILES - 1:
-                done = slice(j + 1 - HALF_TILES, j + 1)
-                nc.sync.dma_start(out=k_view[:, :, done, :], in_=k_stage[:, :, done, :])
-                nc.sync.dma_start(out=v_view[:, :, done, :], in_=v_stage[:, :, done, :])
+        def quantise_for(unit):
+            slot, first, tiles = unit
+            for group in X_QUANTS:
+                if first <= group[0] < first + tiles and group not in quantised_x:
+                    quantised_x.add(group)
+                    quantise_x(group)
+            if chunk_of[slot] not in quantised_w:
+                quantised_w.add(chunk_of[slot])
+                quantise_w(chunk_of[slot])
+
+        for step in range(-LEAD_REGROUP, len(units)):
+            if step + LEAD_REGROUP < len(units):
+                regroup_for(units[step + LEAD_REGROUP])
+            if 0 <= step + LEAD_QUANTISE < len(units):
+                quantise_for(units[step + LEAD_QUANTISE])
+            if 0 <= step + LEAD_MULTIPLY < len(units):
+                accs[step + LEAD_MULTIPLY] = multiply(units[step + LEAD_MULTIPLY])
+            if step >= 0:
+                add = nc.vector.tensor_tensor if step == len(units) - 1 else nc.gpsimd.tensor_tensor
+                finish(units[step], accs[step], add)

@@ -27,36 +27,28 @@ GROUP_SLOTS = QPK + 2
 KEY = QPK
 VALUE = QPK + 1
 BANK_TILES = 4
+BANK = BANK_TILES * HD
+KEY_ROWS = TILES // 2
 
 FLOPS = 2 * TOKENS * K * GROUPS * GROUP_SLOTS * HD
 
-CHUNKS = ((0, 2), (2, 2), (4, 2), (6, 4), (10, 2))
-X_LOADS = ((0,), (1,), (2, 3), (4, 5), (6, 7))
-X_QUANTS = ((0,), (1,), (2, 3), (4, 5, 6, 7))
-HEAD_UNITS = ((0, 0, 1), (0, 1, 1), (1, 0, 2), (0, 2, 2), (1, 2, 2), (2, 0, 4), (3, 0, 4))
-HEAD_REST = ((0, 4, 4), (1, 4, 4), (2, 4, 4), (3, 4, 4))
-LATER_SLOTS = (5, 4, 6, 7, 8, 9, 11, 10)
-LEAD_REGROUP = 5
-LEAD_QUANTISE = 4
-LEAD_MULTIPLY = 2
+CHUNK_SLOTS = 2
+CHUNKS = GROUPS * GROUP_SLOTS // CHUNK_SLOTS
+CHUNK_COLS = CHUNK_SLOTS * HD
+TILE_GROUPS = ((0,), (1,), (2, 3), (4, 5), (6, 7))
+LATER_SLOTS = (2, 3, 4, 6, 7, 5, 8, 9, 11, 10)
+LEAD_TURN = 2
+LEAD_REGROUP = 6
+LEAD_MULTIPLY = 3
+VECTOR_ADDS_EVERY = 8
 
 
 def tile_causalselfattentiongqa_pa_kernel(tc, x, freqs_cis, W_attn, out_0, out_1, out_2):
     nc = tc.nc
-    units = list(HEAD_UNITS) + list(HEAD_REST)
-    for slot in LATER_SLOTS:
-        for first in range(0, TILES, BANK_TILES):
-            units.append((slot, first, BANK_TILES))
-    chunk_of = {}
-    for ch, (first_slot, slots) in enumerate(CHUNKS):
-        for slot in range(first_slot, first_slot + slots):
-            chunk_of[slot] = ch
-
     with ExitStack() as ctx:
         keep = ctx.enter_context(tc.tile_pool(name="keep", bufs=1))
         work = ctx.enter_context(tc.tile_pool(name="work", bufs=6))
-        psum_t = ctx.enter_context(tc.psum_pool(name="psum_t", bufs=2))
-        psum_acc = ctx.enter_context(tc.psum_pool(name="psum_acc", bufs=6))
+        psum = ctx.enter_context(tc.psum_pool(name="psum", bufs=8))
 
         x_view = x.flatten_outer_dims().rearrange("(i j) k -> i (j k)", j=TILES)
         w_view = W_attn.rearrange("(c p t) n -> p c t n", c=PASSES, t=PACK)
@@ -70,7 +62,7 @@ def tile_causalselfattentiongqa_pa_kernel(tc, x, freqs_cis, W_attn, out_0, out_1
             "(g i j) d -> i g j d", g=GROUPS, j=TILES
         )
         q_freqs = freqs_cis.rearrange("(a i) f e -> i a f e", a=GROUPS * QPK)
-        k_freqs = freqs_cis.rearrange("(g i r) f e -> i g r f e", g=GROUPS, r=TILES // 2)
+        k_freqs = freqs_cis.rearrange("(g i r) f e -> i g r f e", g=GROUPS, r=KEY_ROWS)
 
         x_sb = keep.tile([P, TILES * K], BF16)
         x_grouped = keep.tile([P, TILES * K], BF16, align_bytes=64)
@@ -80,58 +72,57 @@ def tile_causalselfattentiongqa_pa_kernel(tc, x, freqs_cis, W_attn, out_0, out_1
         w_grouped = []
         w_codes = []
         w_scales = []
-        for ch, (first_slot, slots) in enumerate(CHUNKS):
-            cols = slots * HD
-            w_raw.append(keep.tile([P, PASSES, PACK, cols], BF16, name="w_raw%d" % ch))
+        for ch in range(CHUNKS):
+            w_raw.append(keep.tile([P, PASSES, PACK, CHUNK_COLS], BF16, name="w_raw%d" % ch))
             w_grouped.append(
-                keep.tile([P, PASSES, cols, PACK], BF16, name="w_grouped%d" % ch, align_bytes=64)
+                keep.tile([P, PASSES, CHUNK_COLS, PACK], BF16, name="w_grouped%d" % ch, align_bytes=64)
             )
-            w_codes.append(keep.tile([P, PASSES, cols], U32, name="w_codes%d" % ch, align_bytes=64))
-            w_scales.append(keep.tile([P, PASSES, cols], U8, name="w_scales%d" % ch, align_bytes=64))
+            w_codes.append(keep.tile([P, PASSES, CHUNK_COLS], U32, name="w_codes%d" % ch, align_bytes=64))
+            w_scales.append(keep.tile([P, PASSES, CHUNK_COLS], U8, name="w_scales%d" % ch, align_bytes=64))
         q_table = keep.tile([P, GROUPS * QPK, 2, HALF, 2], BF16)
-        k_table = keep.tile([P, GROUPS * TILES // 2, 2, HALF, 2], BF16)
+        k_table = keep.tile([P, GROUPS * KEY_ROWS, 2, HALF, 2], BF16)
         identity = keep.tile([P, P], F32)
 
         make_identity(nc, identity[:])
 
-        def load_x(tiles):
-            cols = slice(tiles[0] * K, (tiles[-1] + 1) * K)
+        def load_x(j):
+            cols = slice(j * K, (j + 1) * K)
             nc.sync.dma_start(out=x_sb[:, cols], in_=x_view[:, cols])
 
         def load_w(ch):
-            first_slot, slots = CHUNKS[ch]
             for c in range(PASSES):
                 nc.sync.dma_start(
                     out=w_raw[ch][:, c, :, :],
-                    in_=w_view[:, c, :, first_slot * HD : (first_slot + slots) * HD],
+                    in_=w_view[:, c, :, ch * CHUNK_COLS : (ch + 1) * CHUNK_COLS],
                 )
 
         def load_q_table(g):
             rows = slice(g * QPK, (g + 1) * QPK)
             nc.sync.dma_start(out=q_table[:, rows, 0, :, :], in_=q_freqs[:, rows, :, :])
 
-        load_q_table(0)
-        load_x(X_LOADS[0])
-        load_w(0)
-        load_x(X_LOADS[1])
-        load_x(X_LOADS[2])
-        load_w(1)
-        load_x(X_LOADS[3])
-        load_x(X_LOADS[4])
-        load_w(2)
-        for g in range(GROUPS):
-            rows = slice(g * (TILES // 2), (g + 1) * (TILES // 2))
+        def load_k_table(g):
+            rows = slice(g * KEY_ROWS, (g + 1) * KEY_ROWS)
             nc.sync.dma_start(out=k_table[:, rows, 0, :, :], in_=k_freqs[:, g, :, :, :])
-        load_q_table(1)
+
+        load_q_table(0)
+        load_x(0)
+        load_w(0)
+        for j in range(1, TILES):
+            load_x(j)
+        load_w(1)
+        load_w(2)
+        load_k_table(0)
+        load_k_table(1)
         load_w(3)
+        load_q_table(1)
         load_w(4)
+        load_w(5)
 
         def turn_table(table):
             nc.scalar.activation(out=table[:, :, 1, :, 0], in_=table[:, :, 0, :, 1], func=COPY, scale=-1.0)
             nc.scalar.copy(out=table[:, :, 1, :, 1], in_=table[:, :, 0, :, 0])
 
-        def regroup_w(ch):
-            copy = nc.vector.tensor_copy if ch == 0 else nc.scalar.copy
+        def regroup_w(copy, ch):
             for c in range(PASSES):
                 copy(
                     out=w_grouped[ch][:, c, :, :].rearrange("p (n i) t -> p n t i", i=4),
@@ -150,7 +141,7 @@ def tile_causalselfattentiongqa_pa_kernel(tc, x, freqs_cis, W_attn, out_0, out_1
         )
 
         def turn_x(j):
-            turned = psum_t.tile([P, PASSES * 2, P], F32, tag="turned")
+            turned = psum.tile([P, PASSES * 2, P], F32, tag="bank")
             for c in range(PASSES):
                 for u in range(2):
                     nc.tensor.transpose(turned[:, 2 * c + u, :], x_words[:, j, c, u, :], identity[:])
@@ -169,14 +160,13 @@ def tile_causalselfattentiongqa_pa_kernel(tc, x, freqs_cis, W_attn, out_0, out_1
                 in_=x_grouped[:, first * K : after * K],
             )
 
-        def multiply(unit):
-            slot, first, tiles = unit
-            ch = chunk_of[slot]
-            cols = slice((slot - CHUNKS[ch][0]) * HD, (slot - CHUNKS[ch][0] + 1) * HD)
-            acc = psum_acc.tile([P, BANK_TILES * HD], F32, tag="acc")
-            for n in range(tiles):
+        def multiply(pieces):
+            acc = psum.tile([P, BANK], F32, tag="bank")
+            for n, (slot, j) in enumerate(pieces):
+                ch, at = divmod(slot, CHUNK_SLOTS)
+                cols = slice(at * HD, (at + 1) * HD)
                 for c in range(PASSES):
-                    tokens = slice(((first + n) * PASSES + c) * P, ((first + n) * PASSES + c + 1) * P)
+                    tokens = slice((j * PASSES + c) * P, (j * PASSES + c + 1) * P)
                     nc.tensor.matmul_mx(
                         out=acc[:, n * HD : (n + 1) * HD],
                         lhsT=x_codes[:, tokens].bitcast(FP8X4),
@@ -188,81 +178,111 @@ def tile_causalselfattentiongqa_pa_kernel(tc, x, freqs_cis, W_attn, out_0, out_1
                     )
             return acc
 
-        def products(dest, acc, table, row, first, tiles):
-            shape = [P, 2, tiles, HALF, 2]
-            cols = slice(first * HD, (first + tiles) * HD)
+        def products(both, acc, table, row, first, pieces):
+            shape = [P, 2, pieces, HALF, 2]
+            cols = slice(first * HD, (first + pieces) * HD)
             nc.vector.tensor_tensor(
-                out=dest[:, :, cols].rearrange("p h (j f e) -> p h j f e", f=HALF, e=2),
+                out=both[:, :, cols].rearrange("p h (n f e) -> p h n f e", f=HALF, e=2),
                 in0=acc[:, cols]
-                .rearrange("p (j f h) -> p h j f", f=HALF, h=2)
+                .rearrange("p (n f h) -> p h n f", f=HALF, h=2)
                 .unsqueeze(4)
                 .to_broadcast(shape),
                 in1=table[:, row, :, :, :].unsqueeze(2).to_broadcast(shape),
                 op=MULT,
             )
 
-        def finish(unit, acc, add):
-            slot, first, tiles = unit
-            g, place = divmod(slot, GROUP_SLOTS)
-            width = tiles * HD
-            rows = work.tile([P, BANK_TILES * HD], F32, tag="rows")
-            if place == VALUE:
-                nc.scalar.copy(out=rows[:, :width], in_=acc[:, :width])
-                dest = v_view[:, g, first : first + tiles, :]
-            else:
-                both = work.tile([P, 2, BANK_TILES * HD], F32, tag="both")
-                if place == KEY:
-                    for n in range(0, tiles, 2):
-                        products(both, acc, k_table, g * (TILES // 2) + (first + n) // 2, n, 2)
-                    dest = k_view[:, g, first : first + tiles, :]
-                else:
-                    products(both, acc, q_table, g * QPK + place, 0, tiles)
-                    dest = q_view[:, g * QPK + place, first : first + tiles, :]
-                add(out=rows[:, :width], in0=both[:, 0, :width], in1=both[:, 1, :width], op=ADD)
-            nc.sync.dma_start(out=dest, in_=rows[:, :width].rearrange("p (j d) -> p j d", d=HD))
+        def add_halves(add, both, width):
+            rows = work.tile([P, BANK], F32, tag="rows")
+            add(out=rows[:, :width], in0=both[:, 0, :width], in1=both[:, 1, :width], op=ADD)
+            return rows
 
-        turned_x = set()
-        quantised_x = set()
-        regrouped = set()
-        quantised_w = set()
-        tables = set()
-        accs = {}
-
-        def regroup_for(unit):
-            slot, first, tiles = unit
-            g, place = divmod(slot, GROUP_SLOTS)
-            if place < QPK and ("q", g) not in tables:
-                tables.add(("q", g))
-                rows = slice(g * QPK, (g + 1) * QPK)
-                turn_table(q_table[:, rows, :, :, :])
-            if place == KEY and "k" not in tables:
-                tables.add("k")
-                turn_table(k_table[:])
-            for j in range(first, first + tiles):
-                if j not in turned_x:
-                    turned_x.add(j)
+        with tc.manual_schedule():
+            turn_table(q_table[:, :QPK, :, :, :])
+            for group in TILE_GROUPS[:LEAD_TURN]:
+                for j in group:
                     turn_x(j)
-            if chunk_of[slot] not in regrouped:
-                regrouped.add(chunk_of[slot])
-                regroup_w(chunk_of[slot])
+            regroup_w(nc.vector.tensor_copy, 0)
+            quantise_x(TILE_GROUPS[0])
+            quantise_w(0)
 
-        def quantise_for(unit):
-            slot, first, tiles = unit
-            for group in X_QUANTS:
-                if first <= group[0] < first + tiles and group not in quantised_x:
-                    quantised_x.add(group)
-                    quantise_x(group)
-            if chunk_of[slot] not in quantised_w:
-                quantised_w.add(chunk_of[slot])
-                quantise_w(chunk_of[slot])
+            banks = [(slot, half) for slot in LATER_SLOTS for half in range(TILES // BANK_TILES)]
+            regrouped = set()
+            quantised = set()
+            tables = set()
+            accs = {}
 
-        for step in range(-LEAD_REGROUP, len(units)):
-            if step + LEAD_REGROUP < len(units):
-                regroup_for(units[step + LEAD_REGROUP])
-            if 0 <= step + LEAD_QUANTISE < len(units):
-                quantise_for(units[step + LEAD_QUANTISE])
-            if 0 <= step + LEAD_MULTIPLY < len(units):
-                accs[step + LEAD_MULTIPLY] = multiply(units[step + LEAD_MULTIPLY])
-            if step >= 0:
-                add = nc.vector.tensor_tensor if step == len(units) - 1 else nc.gpsimd.tensor_tensor
-                finish(units[step], accs[step], add)
+            def regroup_for(n):
+                if n >= len(banks):
+                    return
+                slot = banks[n][0]
+                g, place = divmod(slot, GROUP_SLOTS)
+                ch = slot // CHUNK_SLOTS
+                if ch not in regrouped:
+                    regrouped.add(ch)
+                    regroup_w(nc.scalar.copy, ch)
+                if place == KEY and "k" not in tables:
+                    tables.add("k")
+                    turn_table(k_table[:])
+                if place < QPK and g > 0 and "q" not in tables:
+                    tables.add("q")
+                    turn_table(q_table[:, QPK:, :, :, :])
+
+            def multiply_next(n):
+                if n >= len(banks) or n in accs:
+                    return
+                slot, half = banks[n]
+                ch = slot // CHUNK_SLOTS
+                if ch not in quantised:
+                    quantised.add(ch)
+                    quantise_w(ch)
+                accs[n] = multiply([(slot, half * BANK_TILES + j) for j in range(BANK_TILES)])
+
+            steps = len(TILE_GROUPS)
+            for step, group in enumerate(TILE_GROUPS):
+                if step + LEAD_TURN < steps:
+                    for j in TILE_GROUPS[step + LEAD_TURN]:
+                        turn_x(j)
+                if step + 1 < steps:
+                    quantise_x(TILE_GROUPS[step + 1])
+                acc = multiply([(slot, j) for slot in range(CHUNK_SLOTS) for j in group])
+                if step + LEAD_TURN >= steps - 1:
+                    for n in range(step - steps + LEAD_REGROUP + 1):
+                        regroup_for(n)
+                if step == steps - 1:
+                    multiply_next(0)
+                both = work.tile([P, 2, BANK], F32, tag="both")
+                for slot in range(CHUNK_SLOTS):
+                    products(both, acc, q_table, slot, slot * len(group), len(group))
+                width = CHUNK_SLOTS * len(group) * HD
+                rows = add_halves(nc.gpsimd.tensor_tensor, both, width)
+                nc.sync.dma_start(
+                    out=q_view[:, :CHUNK_SLOTS, group[0] : group[-1] + 1, :],
+                    in_=rows[:, :width].rearrange("p (a j d) -> p a j d", a=CHUNK_SLOTS, d=HD),
+                )
+
+            rotated = 0
+            for n, (slot, half) in enumerate(banks):
+                regroup_for(n + LEAD_REGROUP)
+                for ahead in range(1, LEAD_MULTIPLY + 1):
+                    multiply_next(n + ahead)
+                g, place = divmod(slot, GROUP_SLOTS)
+                tiles = slice(half * BANK_TILES, (half + 1) * BANK_TILES)
+                if place == VALUE:
+                    rows = work.tile([P, BANK], F32, tag="rows")
+                    nc.scalar.copy(out=rows[:], in_=accs[n][:])
+                    dest = v_view[:, g, tiles, :]
+                else:
+                    both = work.tile([P, 2, BANK], F32, tag="both")
+                    if place == KEY:
+                        for pair in range(BANK_TILES // 2):
+                            row = g * KEY_ROWS + half * (BANK_TILES // 2) + pair
+                            products(both, accs[n], k_table, row, 2 * pair, 2)
+                        dest = k_view[:, g, tiles, :]
+                    else:
+                        products(both, accs[n], q_table, g * QPK + place, 0, BANK_TILES)
+                        dest = q_view[:, g * QPK + place, tiles, :]
+                    rotated += 1
+                    by_vector = rotated % VECTOR_ADDS_EVERY == 0 or n == len(banks) - 1
+                    add = nc.vector.tensor_tensor if by_vector else nc.gpsimd.tensor_tensor
+                    rows = add_halves(add, both, BANK)
+                nc.sync.dma_start(out=dest, in_=rows[:].rearrange("p (j d) -> p j d", d=HD))

@@ -47,7 +47,7 @@ def tile_causalselfattentiongqa_pa_kernel(tc, x, freqs_cis, W_attn, out_0, out_1
     nc = tc.nc
     with ExitStack() as ctx:
         keep = ctx.enter_context(tc.tile_pool(name="keep", bufs=1))
-        work = ctx.enter_context(tc.tile_pool(name="work", bufs=6))
+        work = ctx.enter_context(tc.tile_pool(name="work", bufs=10))
         psum = ctx.enter_context(tc.psum_pool(name="psum", bufs=8))
 
         x_view = x.flatten_outer_dims().rearrange("(i j) k -> i (j k)", j=TILES)
@@ -110,13 +110,15 @@ def tile_causalselfattentiongqa_pa_kernel(tc, x, freqs_cis, W_attn, out_0, out_1
         for j in range(1, TILES):
             load_x(j)
         load_w(1)
-        load_w(2)
-        load_k_table(0)
-        load_k_table(1)
-        load_w(3)
-        load_q_table(1)
-        load_w(4)
-        load_w(5)
+        later_loads = (
+            (load_w, 2),
+            (load_k_table, 0),
+            (load_k_table, 1),
+            (load_w, 3),
+            (load_q_table, 1),
+            (load_w, 4),
+            (load_w, 5),
+        )
 
         def turn_table(table):
             nc.scalar.activation(out=table[:, :, 1, :, 0], in_=table[:, :, 0, :, 1], func=COPY, scale=-1.0)
@@ -255,6 +257,8 @@ def tile_causalselfattentiongqa_pa_kernel(tc, x, freqs_cis, W_attn, out_0, out_1
                     products(both, acc, q_table, slot, slot * len(group), len(group))
                 width = CHUNK_SLOTS * len(group) * HD
                 rows = add_halves(nc.gpsimd.tensor_tensor, both, width)
+                for load, what in later_loads[2 * step : 2 * step + 2]:
+                    load(what)
                 nc.sync.dma_start(
                     out=q_view[:, :CHUNK_SLOTS, group[0] : group[-1] + 1, :],
                     in_=rows[:, :width].rearrange("p (a j d) -> p a j d", a=CHUNK_SLOTS, d=HD),

@@ -38,9 +38,10 @@ CHUNK_COLS = CHUNK_SLOTS * HD
 TILE_GROUPS = ((0,), (1,), (2, 3), (4, 5), (6, 7))
 LATER_SLOTS = (2, 3, 4, 6, 7, 5, 8, 9, 11, 10)
 LEAD_TURN = 2
-LEAD_REGROUP = 6
+LEAD_REGROUP = 8
 LEAD_MULTIPLY = 3
-VECTOR_ADDS_EVERY = 8
+TENSOR_ADDS_EVERY = 4
+TENSOR_ADD_LAG = 2
 
 
 def tile_causalselfattentiongqa_pa_kernel(tc, x, freqs_cis, W_attn, out_0, out_1, out_2):
@@ -264,11 +265,30 @@ def tile_causalselfattentiongqa_pa_kernel(tc, x, freqs_cis, W_attn, out_0, out_1
                     in_=rows[:, :width].rearrange("p (a j d) -> p a j d", a=CHUNK_SLOTS, d=HD),
                 )
 
+            def add_in_psum(both, dest):
+                total = psum.tile([P, BANK], F32, tag="bank")
+                for h in range(2):
+                    nc.tensor.matmul(
+                        out=total[:], lhsT=identity[:], rhs=both[:, h, :], start=(h == 0), stop=(h == 1)
+                    )
+                return total
+
+            def store_total(total, dest):
+                rows = work.tile([P, BANK], F32, tag="rows")
+                nc.scalar.copy(out=rows[:], in_=total[:])
+                nc.sync.dma_start(out=dest, in_=rows[:].rearrange("p (j d) -> p j d", d=HD))
+
             rotated = 0
+            waiting = {}
+            totals = {}
             for n, (slot, half) in enumerate(banks):
+                if n - 1 in totals:
+                    store_total(totals[n - 1][0], totals[n - 1][1])
                 regroup_for(n + LEAD_REGROUP)
                 for ahead in range(1, LEAD_MULTIPLY + 1):
                     multiply_next(n + ahead)
+                if n - TENSOR_ADD_LAG in waiting:
+                    totals[n] = (add_in_psum(waiting[n - TENSOR_ADD_LAG][0], waiting[n - TENSOR_ADD_LAG][1]), waiting[n - TENSOR_ADD_LAG][1])
                 g, place = divmod(slot, GROUP_SLOTS)
                 tiles = slice(half * BANK_TILES, (half + 1) * BANK_TILES)
                 if place == VALUE:
@@ -286,7 +306,11 @@ def tile_causalselfattentiongqa_pa_kernel(tc, x, freqs_cis, W_attn, out_0, out_1
                         products(both, accs[n], q_table, g * QPK + place, 0, BANK_TILES)
                         dest = q_view[:, g * QPK + place, tiles, :]
                     rotated += 1
-                    by_vector = rotated % VECTOR_ADDS_EVERY == 0 or n == len(banks) - 1
-                    add = nc.vector.tensor_tensor if by_vector else nc.gpsimd.tensor_tensor
-                    rows = add_halves(add, both, BANK)
+                    if n == len(banks) - 1:
+                        rows = add_halves(nc.vector.tensor_tensor, both, BANK)
+                    elif rotated % TENSOR_ADDS_EVERY == 0 and n + TENSOR_ADD_LAG + 1 < len(banks):
+                        waiting[n] = (both, dest)
+                        continue
+                    else:
+                        rows = add_halves(nc.gpsimd.tensor_tensor, both, BANK)
                 nc.sync.dma_start(out=dest, in_=rows[:].rearrange("p (j d) -> p j d", d=HD))

@@ -39,8 +39,9 @@ TILE_GROUPS = ((0,), (1,), (2, 3), (4, 5), (6, 7))
 LATER_SLOTS = (2, 3, 4, 6, 7, 5, 8, 9, 11, 10)
 LEAD_TURN = 2
 LEAD_REGROUP = 8
-LEAD_MULTIPLY = 3
+LEAD_MULTIPLY = 4
 TENSOR_ADDS_EVERY = 4
+TENSOR_ADDS_END = 8
 TENSOR_ADD_LAG = 2
 
 
@@ -308,7 +309,7 @@ def tile_causalselfattentiongqa_pa_kernel(tc, x, freqs_cis, W_attn, out_0, out_1
                     rotated += 1
                     if n == len(banks) - 1:
                         rows = add_halves(nc.vector.tensor_tensor, both, BANK)
-                    elif rotated % TENSOR_ADDS_EVERY == 0 and n + TENSOR_ADD_LAG + 1 < len(banks):
+                    elif rotated % TENSOR_ADDS_EVERY == 0 and n + TENSOR_ADDS_END < len(banks):
                         waiting[n] = (both, dest)
                         continue
                     else:

@@ -63,8 +63,8 @@ def tile_causalselfattentiongqa_pa_kernel(tc, x, freqs_cis, W_attn, out_0, out_1
         v_view = out_2.rearrange("o n h d -> (o n h) d").rearrange(
             "(g i j) d -> i g j d", g=GROUPS, j=TILES
         )
-        q_freqs = freqs_cis.rearrange("(a i) f e -> i a f e", a=GROUPS * QPK)
-        k_freqs = freqs_cis.rearrange("(g i r) f e -> i g r f e", g=GROUPS, r=KEY_ROWS)
+        q_freqs = freqs_cis.rearrange("(a i) f e -> i a (f e)", a=GROUPS * QPK)
+        k_freqs = freqs_cis.rearrange("(g i r) f e -> i g r (f e)", g=GROUPS, r=KEY_ROWS)
 
         x_sb = keep.tile([P, TILES * K], BF16)
         x_grouped = keep.tile([P, TILES * K], BF16, align_bytes=64)
@@ -81,8 +81,11 @@ def tile_causalselfattentiongqa_pa_kernel(tc, x, freqs_cis, W_attn, out_0, out_1
             )
             w_codes.append(keep.tile([P, PASSES, CHUNK_COLS], U32, name="w_codes%d" % ch, align_bytes=64))
             w_scales.append(keep.tile([P, PASSES, CHUNK_COLS], U8, name="w_scales%d" % ch, align_bytes=64))
-        q_table = keep.tile([P, GROUPS * QPK, 2, HALF, 2], BF16)
-        k_table = keep.tile([P, GROUPS * KEY_ROWS, 2, HALF, 2], BF16)
+        q_table = []
+        k_table = []
+        for g in range(GROUPS):
+            q_table.append(keep.tile([P, 2, QPK, HD], BF16, name="q_table%d" % g))
+            k_table.append(keep.tile([P, 2, KEY_ROWS, HD], BF16, name="k_table%d" % g))
         identity = keep.tile([P, P], F32)
 
         make_identity(nc, identity[:])
@@ -99,12 +102,10 @@ def tile_causalselfattentiongqa_pa_kernel(tc, x, freqs_cis, W_attn, out_0, out_1
                 )
 
         def load_q_table(g):
-            rows = slice(g * QPK, (g + 1) * QPK)
-            nc.sync.dma_start(out=q_table[:, rows, 0, :, :], in_=q_freqs[:, rows, :, :])
+            nc.sync.dma_start(out=q_table[g][:, 0, :, :], in_=q_freqs[:, g * QPK : (g + 1) * QPK, :])
 
         def load_k_table(g):
-            rows = slice(g * KEY_ROWS, (g + 1) * KEY_ROWS)
-            nc.sync.dma_start(out=k_table[:, rows, 0, :, :], in_=k_freqs[:, g, :, :, :])
+            nc.sync.dma_start(out=k_table[g][:, 0, :, :], in_=k_freqs[:, g, :, :])
 
         load_q_table(0)
         load_x(0)
@@ -123,8 +124,10 @@ def tile_causalselfattentiongqa_pa_kernel(tc, x, freqs_cis, W_attn, out_0, out_1
         )
 
         def turn_table(table):
-            nc.scalar.activation(out=table[:, :, 1, :, 0], in_=table[:, :, 0, :, 1], func=COPY, scale=-1.0)
-            nc.scalar.copy(out=table[:, :, 1, :, 1], in_=table[:, :, 0, :, 0])
+            loaded = table[:, 0, :, :].rearrange("p r (f e) -> p r f e", e=2)
+            turned = table[:, 1, :, :].rearrange("p r (f e) -> p r f e", e=2)
+            nc.scalar.activation(out=turned[:, :, :, 0], in_=loaded[:, :, :, 1], func=COPY, scale=-1.0)
+            nc.scalar.copy(out=turned[:, :, :, 1], in_=loaded[:, :, :, 0])
 
         def regroup_w(copy, ch):
             for c in range(PASSES):
@@ -182,26 +185,35 @@ def tile_causalselfattentiongqa_pa_kernel(tc, x, freqs_cis, W_attn, out_0, out_1
                     )
             return acc
 
-        def products(both, acc, table, row, first, pieces):
-            shape = [P, 2, pieces, HALF, 2]
-            cols = slice(first * HD, (first + pieces) * HD)
+        def products(both, acc, table, first, positions, repeats):
+            width = repeats * positions * HD
+            shape = [P, 2, repeats, positions * HALF, 2]
             nc.vector.tensor_tensor(
-                out=both[:, :, cols].rearrange("p h (n f e) -> p h n f e", f=HALF, e=2),
-                in0=acc[:, cols]
-                .rearrange("p (n f h) -> p h n f", f=HALF, h=2)
+                out=both[:, :, :width].rearrange("p h (j q e) -> p h j q e", j=repeats, e=2),
+                in0=acc[:, :width]
+                .rearrange("p (j q h) -> p h j q", j=repeats, h=2)
                 .unsqueeze(4)
                 .to_broadcast(shape),
-                in1=table[:, row, :, :, :].unsqueeze(2).to_broadcast(shape),
+                in1=table[:, :, first : first + positions, :]
+                .rearrange("p h r (f e) -> p h (r f) e", e=2)
+                .unsqueeze(2)
+                .to_broadcast(shape),
                 op=MULT,
             )
 
-        def add_halves(add, both, width):
+        def add_halves(add, both, positions, repeats):
+            width = repeats * positions * HD
             rows = work.tile([P, BANK], F32, tag="rows")
-            add(out=rows[:, :width], in0=both[:, 0, :width], in1=both[:, 1, :width], op=ADD)
+            add(
+                out=rows[:, :width].rearrange("p (r j d) -> p j r d", r=positions, d=HD),
+                in0=both[:, 0, :width].rearrange("p (j r d) -> p j r d", r=positions, d=HD),
+                in1=both[:, 1, :width].rearrange("p (j r d) -> p j r d", r=positions, d=HD),
+                op=ADD,
+            )
             return rows
 
         with tc.manual_schedule():
-            turn_table(q_table[:, :QPK, :, :, :])
+            turn_table(q_table[0])
             for group in TILE_GROUPS[:LEAD_TURN]:
                 for j in group:
                     turn_x(j)
@@ -224,12 +236,12 @@ def tile_causalselfattentiongqa_pa_kernel(tc, x, freqs_cis, W_attn, out_0, out_1
                 if ch not in regrouped:
                     regrouped.add(ch)
                     regroup_w(nc.scalar.copy, ch)
-                if place == KEY and "k" not in tables:
-                    tables.add("k")
-                    turn_table(k_table[:])
-                if place < QPK and g > 0 and "q" not in tables:
-                    tables.add("q")
-                    turn_table(q_table[:, QPK:, :, :, :])
+                if place == KEY and ("k", g) not in tables:
+                    tables.add(("k", g))
+                    turn_table(k_table[g])
+                if place < QPK and g > 0 and ("q", g) not in tables:
+                    tables.add(("q", g))
+                    turn_table(q_table[g])
 
             def multiply_next(n):
                 if n >= len(banks) or n in accs:
@@ -239,7 +251,12 @@ def tile_causalselfattentiongqa_pa_kernel(tc, x, freqs_cis, W_attn, out_0, out_1
                 if ch not in quantised:
                     quantised.add(ch)
                     quantise_w(ch)
-                accs[n] = multiply([(slot, half * BANK_TILES + j) for j in range(BANK_TILES)])
+                first = half * BANK_TILES
+                if slot % GROUP_SLOTS == KEY:
+                    tiles = [first + 2 * r + j for j in range(2) for r in range(BANK_TILES // 2)]
+                else:
+                    tiles = [first + j for j in range(BANK_TILES)]
+                accs[n] = multiply([(slot, j) for j in tiles])
 
             steps = len(TILE_GROUPS)
             for step, group in enumerate(TILE_GROUPS):
@@ -248,17 +265,16 @@ def tile_causalselfattentiongqa_pa_kernel(tc, x, freqs_cis, W_attn, out_0, out_1
                         turn_x(j)
                 if step + 1 < steps:
                     quantise_x(TILE_GROUPS[step + 1])
-                acc = multiply([(slot, j) for slot in range(CHUNK_SLOTS) for j in group])
+                acc = multiply([(slot, j) for j in group for slot in range(CHUNK_SLOTS)])
                 if step + LEAD_TURN >= steps - 1:
                     for n in range(step - steps + LEAD_REGROUP + 1):
                         regroup_for(n)
                 if step == steps - 1:
                     multiply_next(0)
                 both = work.tile([P, 2, BANK], F32, tag="both")
-                for slot in range(CHUNK_SLOTS):
-                    products(both, acc, q_table, slot, slot * len(group), len(group))
+                products(both, acc, q_table[0], 0, CHUNK_SLOTS, len(group))
                 width = CHUNK_SLOTS * len(group) * HD
-                rows = add_halves(nc.gpsimd.tensor_tensor, both, width)
+                rows = add_halves(nc.gpsimd.tensor_tensor, both, CHUNK_SLOTS, len(group))
                 for load, what in later_loads[2 * step : 2 * step + 2]:
                     load(what)
                 nc.sync.dma_start(
@@ -299,19 +315,19 @@ def tile_causalselfattentiongqa_pa_kernel(tc, x, freqs_cis, W_attn, out_0, out_1
                 else:
                     both = work.tile([P, 2, BANK], F32, tag="both")
                     if place == KEY:
-                        for pair in range(BANK_TILES // 2):
-                            row = g * KEY_ROWS + half * (BANK_TILES // 2) + pair
-                            products(both, accs[n], k_table, row, 2 * pair, 2)
+                        positions = BANK_TILES // 2
+                        products(both, accs[n], k_table[g], half * positions, positions, 2)
                         dest = k_view[:, g, tiles, :]
                     else:
-                        products(both, accs[n], q_table, g * QPK + place, 0, BANK_TILES)
+                        positions = 1
+                        products(both, accs[n], q_table[g], place, positions, BANK_TILES)
                         dest = q_view[:, g * QPK + place, tiles, :]
                     rotated += 1
                     if n == len(banks) - 1:
-                        rows = add_halves(nc.vector.tensor_tensor, both, BANK)
-                    elif rotated % TENSOR_ADDS_EVERY == 0 and n + TENSOR_ADDS_END < len(banks):
+                        rows = add_halves(nc.vector.tensor_tensor, both, positions, BANK_TILES // positions)
+                    elif place < QPK and rotated % TENSOR_ADDS_EVERY == 0 and n + TENSOR_ADDS_END < len(banks):
                         waiting[n] = (both, dest)
                         continue
                     else:
-                        rows = add_halves(nc.gpsimd.tensor_tensor, both, BANK)
+                        rows = add_halves(nc.gpsimd.tensor_tensor, both, positions, BANK_TILES // positions)
                 nc.sync.dma_start(out=dest, in_=rows[:].rearrange("p (j d) -> p j d", d=HD))

@@ -10,6 +10,7 @@ U8 = mybir.dt.uint8
 FP8X4 = mybir.dt.float8_e4m3fn_x4
 MULT = mybir.AluOpType.mult
 ADD = mybir.AluOpType.add
+SUB = mybir.AluOpType.subtract
 COPY = mybir.ActivationFunctionType.Copy
 
 P = 128
@@ -35,13 +36,14 @@ FLOPS = 2 * TOKENS * K * GROUPS * GROUP_SLOTS * HD
 CHUNK_SLOTS = 2
 CHUNKS = GROUPS * GROUP_SLOTS // CHUNK_SLOTS
 CHUNK_COLS = CHUNK_SLOTS * HD
-TILE_GROUPS = ((0,), (1,), (2, 3), (4, 5), (6, 7))
-LATER_SLOTS = (2, 3, 4, 6, 7, 5, 8, 9, 11, 10)
-LEAD_TURN = 2
+PAIR_TILES = 2
+QUANTISED_TOGETHER = ((0,), (1,), (2,), (3,), (4,), (5,))
+SPLIT = (1,)
+UNITS = (("split", 1), ("key", 4), ("query", 6), ("query", 7), ("value", 5), ("query", 8), ("query", 9), ("value", 11), ("key", 10))
+TENSOR_ADDS = (6, 9,)
+VECTOR_ADDS = ()
 LEAD_REGROUP = 8
-LEAD_MULTIPLY = 4
-TENSOR_ADDS_EVERY = 4
-TENSOR_ADDS_END = 8
+LEAD_MULTIPLY = 3
 TENSOR_ADD_LAG = 2
 
 
@@ -49,7 +51,7 @@ def tile_causalselfattentiongqa_pa_kernel(tc, x, freqs_cis, W_attn, out_0, out_1
     nc = tc.nc
     with ExitStack() as ctx:
         keep = ctx.enter_context(tc.tile_pool(name="keep", bufs=1))
-        work = ctx.enter_context(tc.tile_pool(name="work", bufs=10))
+        work = ctx.enter_context(tc.tile_pool(name="work", bufs=8))
         psum = ctx.enter_context(tc.psum_pool(name="psum", bufs=8))
 
         x_view = x.flatten_outer_dims().rearrange("(i j) k -> i (j k)", j=TILES)
@@ -76,19 +78,32 @@ def tile_causalselfattentiongqa_pa_kernel(tc, x, freqs_cis, W_attn, out_0, out_1
         w_scales = []
         for ch in range(CHUNKS):
             w_raw.append(keep.tile([P, PASSES, PACK, CHUNK_COLS], BF16, name="w_raw%d" % ch))
-            w_grouped.append(
-                keep.tile([P, PASSES, CHUNK_COLS, PACK], BF16, name="w_grouped%d" % ch, align_bytes=64)
-            )
-            w_codes.append(keep.tile([P, PASSES, CHUNK_COLS], U32, name="w_codes%d" % ch, align_bytes=64))
-            w_scales.append(keep.tile([P, PASSES, CHUNK_COLS], U8, name="w_scales%d" % ch, align_bytes=64))
+        w_grouped = {}
+        w_codes = {}
+        w_scales = {}
+        w_sets = {}
+        for chunks in QUANTISED_TOGETHER:
+            grouped = keep.tile([P, len(chunks), PASSES, CHUNK_COLS, PACK], BF16, name="w_grouped%d" % chunks[0], align_bytes=64)
+            codes = keep.tile([P, len(chunks), PASSES, CHUNK_COLS], U32, name="w_codes%d" % chunks[0], align_bytes=64)
+            scales = keep.tile([P, len(chunks), PASSES, CHUNK_COLS], U8, name="w_scales%d" % chunks[0], align_bytes=64)
+            for n, ch in enumerate(chunks):
+                w_grouped[ch] = grouped[:, n]
+                w_codes[ch] = codes[:, n]
+                w_scales[ch] = scales[:, n]
+                w_sets[ch] = (chunks, grouped, codes, scales)
         q_table = []
         k_table = []
         for g in range(GROUPS):
             q_table.append(keep.tile([P, 2, QPK, HD], BF16, name="q_table%d" % g))
             k_table.append(keep.tile([P, 2, KEY_ROWS, HD], BF16, name="k_table%d" % g))
+        q_mixed = {}
+        for ch in SPLIT:
+            q_mixed[ch] = keep.tile([P, 2, CHUNK_SLOTS * HALF], F32, name="q_mixed%d" % ch)
         identity = keep.tile([P, P], F32)
+        minus = keep.tile([P, P], F32)
 
         make_identity(nc, identity[:])
+        nc.scalar.activation(out=minus[:], in_=identity[:], func=COPY, scale=-1.0)
 
         def load_x(j):
             cols = slice(j * K, (j + 1) * K)
@@ -101,6 +116,9 @@ def tile_causalselfattentiongqa_pa_kernel(tc, x, freqs_cis, W_attn, out_0, out_1
                     in_=w_view[:, c, :, ch * CHUNK_COLS : (ch + 1) * CHUNK_COLS],
                 )
 
+        def load_w_pass(ch, c):
+            nc.sync.dma_start(out=w_raw[ch][:, c, :, :], in_=w_view[:, c, :, ch * CHUNK_COLS : (ch + 1) * CHUNK_COLS])
+
         def load_q_table(g):
             nc.sync.dma_start(out=q_table[g][:, 0, :, :], in_=q_freqs[:, g * QPK : (g + 1) * QPK, :])
 
@@ -110,18 +128,21 @@ def tile_causalselfattentiongqa_pa_kernel(tc, x, freqs_cis, W_attn, out_0, out_1
         load_q_table(0)
         load_x(0)
         load_w(0)
-        for j in range(1, TILES):
-            load_x(j)
+        load_x(1)
+        load_x(2)
+        load_x(3)
+        load_x(4)
+        load_x(5)
+        load_x(6)
+        load_x(7)
         load_w(1)
-        later_loads = (
-            (load_w, 2),
-            (load_k_table, 0),
-            (load_k_table, 1),
-            (load_w, 3),
-            (load_q_table, 1),
-            (load_w, 4),
-            (load_w, 5),
-        )
+        later_loads = ((load_w, 2), (load_k_table, 0), (load_w, 3), (load_q_table, 1), (load_k_table, 1), (load_w, 4), (load_w, 5),)
+
+        def mix_table(ch):
+            g, place = divmod(ch * CHUNK_SLOTS, GROUP_SLOTS)
+            loaded = q_table[g][:, 0, place : place + CHUNK_SLOTS, :].rearrange("p r (f e) -> p (r f) e", e=2)
+            nc.gpsimd.tensor_tensor(out=q_mixed[ch][:, 0, :], in0=loaded[:, :, 0], in1=loaded[:, :, 1], op=ADD)
+            nc.gpsimd.tensor_tensor(out=q_mixed[ch][:, 1, :], in0=loaded[:, :, 0], in1=loaded[:, :, 1], op=SUB)
 
         def turn_table(table):
             loaded = table[:, 0, :, :].rearrange("p r (f e) -> p r f e", e=2)
@@ -129,18 +150,29 @@ def tile_causalselfattentiongqa_pa_kernel(tc, x, freqs_cis, W_attn, out_0, out_1
             nc.scalar.activation(out=turned[:, :, :, 0], in_=loaded[:, :, :, 1], func=COPY, scale=-1.0)
             nc.scalar.copy(out=turned[:, :, :, 1], in_=loaded[:, :, :, 0])
 
-        def regroup_w(copy, ch):
-            for c in range(PASSES):
+        def regroup_pass(copy, ch, c):
+            if ch in SPLIT:
+                for e in range(2):
+                    copy(
+                        out=w_grouped[ch][:, c, e * HD : (e + 1) * HD, :].rearrange("p (n i) t -> p n t i", i=4),
+                        in_=w_raw[ch][:, c, :, :].rearrange("p t (n i e) -> p e n t i", i=4, e=2)[:, 1 - e],
+                    )
+            else:
                 copy(
                     out=w_grouped[ch][:, c, :, :].rearrange("p (n i) t -> p n t i", i=4),
                     in_=w_raw[ch][:, c, :, :].rearrange("p t (n i) -> p n t i", i=4),
                 )
 
+        def regroup_w(copy, ch):
+            for c in range(PASSES):
+                regroup_pass(copy, ch, c)
+
         def quantise_w(ch):
+            grouped, codes, scales = w_sets[ch][1:]
             nc.vector.quantize_mx(
-                out=w_codes[ch][:].rearrange("p c n -> p (c n)").bitcast(FP8X4),
-                scales=w_scales[ch][:].rearrange("p c n -> p (c n)"),
-                in_=w_grouped[ch][:].rearrange("p c n t -> p (c n t)"),
+                out=codes[:].rearrange("p h c n -> p (h c n)").bitcast(FP8X4),
+                scales=scales[:].rearrange("p h c n -> p (h c n)"),
+                in_=grouped[:].rearrange("p h c n t -> p (h c n t)"),
             )
 
         x_words = x_sb[:].bitcast(F32).rearrange(
@@ -185,6 +217,24 @@ def tile_causalselfattentiongqa_pa_kernel(tc, x, freqs_cis, W_attn, out_0, out_1
                     )
             return acc
 
+        def multiply_wide(ch, terms, tiles):
+            acc = psum.tile([P, BANK], F32, tag="bank")
+            width = terms[0].stop - terms[0].start
+            for n, j in enumerate(tiles):
+                passes = [(c, cols) for c in range(PASSES) for cols in terms]
+                for m, (c, cols) in enumerate(passes):
+                    tokens = slice((j * PASSES + c) * P, (j * PASSES + c + 1) * P)
+                    nc.tensor.matmul_mx(
+                        out=acc[:, n * width : (n + 1) * width],
+                        lhsT=x_codes[:, tokens].bitcast(FP8X4),
+                        lhsT_scale=x_scales[:, tokens],
+                        rhs=w_codes[ch][:, c, cols].bitcast(FP8X4),
+                        rhs_scale=w_scales[ch][:, c, cols],
+                        start=(m == 0),
+                        stop=(m == len(passes) - 1),
+                    )
+            return acc
+
         def products(both, acc, table, first, positions, repeats):
             width = repeats * positions * HD
             shape = [P, 2, repeats, positions * HALF, 2]
@@ -213,121 +263,231 @@ def tile_causalselfattentiongqa_pa_kernel(tc, x, freqs_cis, W_attn, out_0, out_1
             return rows
 
         with tc.manual_schedule():
-            turn_table(q_table[0])
-            for group in TILE_GROUPS[:LEAD_TURN]:
-                for j in group:
-                    turn_x(j)
-            regroup_w(nc.vector.tensor_copy, 0)
-            quantise_x(TILE_GROUPS[0])
-            quantise_w(0)
-
-            banks = [(slot, half) for slot in LATER_SLOTS for half in range(TILES // BANK_TILES)]
+            banks = []
+            for kind, what in UNITS:
+                for half in range(TILES // BANK_TILES):
+                    if kind == "split":
+                        banks.append(("sum", what, half, 0))
+                        banks.append(("pair", what, half, 0))
+                        banks.append(("pair", what, half, 1))
+                    else:
+                        banks.append((kind, what, half, 0))
             regrouped = set()
             quantised = set()
             tables = set()
             accs = {}
 
+            def chunk_of(n):
+                kind, what = banks[n][:2]
+                return what if kind in ("sum", "pair") else what // CHUNK_SLOTS
+
             def regroup_for(n):
                 if n >= len(banks):
                     return
-                slot = banks[n][0]
-                g, place = divmod(slot, GROUP_SLOTS)
-                ch = slot // CHUNK_SLOTS
+                kind, what = banks[n][:2]
+                ch = chunk_of(n)
                 if ch not in regrouped:
                     regrouped.add(ch)
                     regroup_w(nc.scalar.copy, ch)
-                if place == KEY and ("k", g) not in tables:
+                g = ch * CHUNK_SLOTS // GROUP_SLOTS
+                if kind == "key" and ("k", g) not in tables:
                     tables.add(("k", g))
                     turn_table(k_table[g])
-                if place < QPK and g > 0 and ("q", g) not in tables:
+                if kind == "query" and g > 0 and ("q", g) not in tables:
                     tables.add(("q", g))
                     turn_table(q_table[g])
+
+            def quantise_for(ch):
+                if ch not in quantised:
+                    for other in w_sets[ch][0]:
+                        quantised.add(other)
+                    quantise_w(ch)
+
+            def quantise_next():
+                for n in range(len(banks)):
+                    if chunk_of(n) not in quantised:
+                        quantise_for(chunk_of(n))
+                        return
 
             def multiply_next(n):
                 if n >= len(banks) or n in accs:
                     return
-                slot, half = banks[n]
-                ch = slot // CHUNK_SLOTS
-                if ch not in quantised:
-                    quantised.add(ch)
-                    quantise_w(ch)
+                kind, what, half, part = banks[n]
+                quantise_for(chunk_of(n))
                 first = half * BANK_TILES
-                if slot % GROUP_SLOTS == KEY:
-                    tiles = [first + 2 * r + j for j in range(2) for r in range(BANK_TILES // 2)]
+                if kind == "sum":
+                    accs[n] = multiply_wide(what, (slice(0, HD), slice(HD, 2 * HD)), range(first, first + BANK_TILES))
+                elif kind == "pair":
+                    first += part * PAIR_TILES
+                    accs[n] = multiply_wide(what, (slice(0, 2 * HD),), range(first, first + PAIR_TILES))
+                elif kind == "key":
+                    accs[n] = multiply([(what, first + 2 * r + j) for j in range(2) for r in range(BANK_TILES // 2)])
                 else:
-                    tiles = [first + j for j in range(BANK_TILES)]
-                accs[n] = multiply([(slot, j) for j in tiles])
+                    accs[n] = multiply([(what, first + j) for j in range(BANK_TILES)])
 
-            steps = len(TILE_GROUPS)
-            for step, group in enumerate(TILE_GROUPS):
-                if step + LEAD_TURN < steps:
-                    for j in TILE_GROUPS[step + LEAD_TURN]:
-                        turn_x(j)
-                if step + 1 < steps:
-                    quantise_x(TILE_GROUPS[step + 1])
-                acc = multiply([(slot, j) for j in group for slot in range(CHUNK_SLOTS)])
-                if step + LEAD_TURN >= steps - 1:
-                    for n in range(step - steps + LEAD_REGROUP + 1):
-                        regroup_for(n)
-                if step == steps - 1:
-                    multiply_next(0)
+            def rotate(ch, acc, group, add):
                 both = work.tile([P, 2, BANK], F32, tag="both")
-                products(both, acc, q_table[0], 0, CHUNK_SLOTS, len(group))
+                products(both, acc, q_table[0], ch * CHUNK_SLOTS, CHUNK_SLOTS, len(group))
+                rows = add_halves(add, both, CHUNK_SLOTS, len(group))
+                return (ch, rows, group)
+
+            def store(what):
+                ch, rows, group = what
                 width = CHUNK_SLOTS * len(group) * HD
-                rows = add_halves(nc.gpsimd.tensor_tensor, both, CHUNK_SLOTS, len(group))
-                for load, what in later_loads[2 * step : 2 * step + 2]:
-                    load(what)
                 nc.sync.dma_start(
-                    out=q_view[:, :CHUNK_SLOTS, group[0] : group[-1] + 1, :],
+                    out=q_view[:, ch * CHUNK_SLOTS : (ch + 1) * CHUNK_SLOTS, group[0] : group[-1] + 1, :],
                     in_=rows[:, :width].rearrange("p (a j d) -> p a j d", a=CHUNK_SLOTS, d=HD),
                 )
 
-            def add_in_psum(both, dest):
+            def later(first, after):
+                for load, what in later_loads[first:after]:
+                    load(what)
+
+            def regroup_first(count):
+                for n in range(count):
+                    regroup_for(n)
+
+            G = nc.gpsimd.tensor_tensor
+            V = nc.vector.tensor_tensor
+            W0 = (slice(0, 2 * HD),)
+            mix_table(1)
+            turn_table(q_table[0])
+            turn_x(0)
+            turn_x(1)
+            regroup_w(nc.vector.tensor_copy, 0)
+            quantise_x((0,))
+            quantise_w(0)
+            turn_x(2)
+            turn_x(3)
+            quantise_x((1,))
+            a = multiply_wide(0, W0, (0,))
+            r = rotate(0, a, (0,), G)
+            later(0, 2)
+            store(r)
+            turn_x(4)
+            turn_x(5)
+            quantise_x((2, 3))
+            a = multiply_wide(0, W0, (1,))
+            r = rotate(0, a, (1,), G)
+            later(2, 4)
+            store(r)
+            turn_x(6)
+            turn_x(7)
+            quantise_x((4, 5))
+            a = multiply_wide(0, W0, (2, 3))
+            regroup_first(LEAD_REGROUP - 2)
+            r = rotate(0, a, (2, 3), G)
+            later(4, 6)
+            store(r)
+            quantise_x((6, 7))
+            a = multiply_wide(0, W0, (4, 5))
+            regroup_first(LEAD_REGROUP - 1)
+            r = rotate(0, a, (4, 5), G)
+            later(6, 7)
+            store(r)
+            a = multiply_wide(0, W0, (6, 7))
+            regroup_first(LEAD_REGROUP)
+            multiply_next(0)
+            r = rotate(0, a, (6, 7), G)
+            store(r)
+
+            def sum_product(acc, cos):
+                prod = work.tile([P, BANK], F32, tag="sum", bufs=4)
+                shape = [P, BANK_TILES, HD]
+                nc.vector.tensor_tensor(
+                    out=prod[:].rearrange("p (j q) -> p j q", q=HD),
+                    in0=acc[:].rearrange("p (j q) -> p j q", q=HD),
+                    in1=cos.unsqueeze(1).to_broadcast(shape),
+                    op=MULT,
+                )
+                return prod
+
+            def pair_product(acc, mixed):
+                prod = work.tile([P, BANK], F32, tag="pair")
+                shape = [P, PAIR_TILES, HD, 2]
+                nc.vector.tensor_tensor(
+                    out=prod[:].rearrange("p (j q e) -> p j q e", j=PAIR_TILES, e=2),
+                    in0=acc[:].rearrange("p (j e q) -> p j q e", j=PAIR_TILES, e=2),
+                    in1=mixed.rearrange("p e q -> p q e").unsqueeze(1).to_broadcast(shape),
+                    op=MULT,
+                )
+                return prod
+
+            def pair_views(rows, part, sums, pair):
+                shape = [P, PAIR_TILES, CHUNK_SLOTS, HALF, 2]
+                return (
+                    rows[:].rearrange("p (s j f e) -> p j s f e", j=PAIR_TILES, f=HALF, e=2),
+                    sums[:, part * PAIR_TILES * HD : (part + 1) * PAIR_TILES * HD]
+                    .rearrange("p (j s f) -> p j s f", j=PAIR_TILES, s=CHUNK_SLOTS)
+                    .unsqueeze(4)
+                    .to_broadcast(shape),
+                    pair[:].rearrange("p (j s f e) -> p j s f e", j=PAIR_TILES, s=CHUNK_SLOTS, e=2),
+                )
+
+            def add_in_psum(terms):
                 total = psum.tile([P, BANK], F32, tag="bank")
-                for h in range(2):
-                    nc.tensor.matmul(
-                        out=total[:], lhsT=identity[:], rhs=both[:, h, :], start=(h == 0), stop=(h == 1)
-                    )
+                for n, (factor, term) in enumerate(terms):
+                    nc.tensor.matmul(out=total[:], lhsT=factor[:], rhs=term, start=(n == 0), stop=(n == 1))
                 return total
 
-            def store_total(total, dest):
-                rows = work.tile([P, BANK], F32, tag="rows")
-                nc.scalar.copy(out=rows[:], in_=total[:])
-                nc.sync.dma_start(out=dest, in_=rows[:].rearrange("p (j d) -> p j d", d=HD))
-
-            rotated = 0
             waiting = {}
             totals = {}
-            for n, (slot, half) in enumerate(banks):
+            sums = {}
+            split_rows = {}
+            for n, (kind, what, half, part) in enumerate(banks):
                 if n - 1 in totals:
-                    store_total(totals[n - 1][0], totals[n - 1][1])
+                    total, order, dest = totals[n - 1]
+                    rows = work.tile([P, BANK], F32, tag="rows")
+                    nc.scalar.copy(out=rows[:].rearrange("p (a b d) -> p b a d", a=order, d=HD), in_=total[:].rearrange("p (b a d) -> p b a d", a=order, d=HD))
+                    dest(rows)
                 regroup_for(n + LEAD_REGROUP)
                 for ahead in range(1, LEAD_MULTIPLY + 1):
                     multiply_next(n + ahead)
                 if n - TENSOR_ADD_LAG in waiting:
-                    totals[n] = (add_in_psum(waiting[n - TENSOR_ADD_LAG][0], waiting[n - TENSOR_ADD_LAG][1]), waiting[n - TENSOR_ADD_LAG][1])
-                g, place = divmod(slot, GROUP_SLOTS)
+                    terms, order, dest = waiting[n - TENSOR_ADD_LAG]
+                    totals[n] = (add_in_psum(terms), order, dest)
+                ch = chunk_of(n)
+                g, place = divmod(ch * CHUNK_SLOTS if kind in ("sum", "pair") else what, GROUP_SLOTS)
                 tiles = slice(half * BANK_TILES, (half + 1) * BANK_TILES)
-                if place == VALUE:
+                add = V if n == len(banks) - 1 or n in VECTOR_ADDS else G
+                if kind == "sum":
+                    cos = q_table[g][:, 0, place : place + CHUNK_SLOTS, :].rearrange("p r (f e) -> p (r f) e", e=2)[:, :, 0]
+                    sums[ch, half] = sum_product(accs[n], cos)
+                elif kind == "pair":
+                    pair = pair_product(accs[n], q_mixed[ch][:])
+                    first = half * BANK_TILES + part * PAIR_TILES
+                    view = q_view[:, g * QPK + place : g * QPK + place + CHUNK_SLOTS, first : first + PAIR_TILES, :]
+
+                    def dest(rows, view=view):
+                        nc.sync.dma_start(out=view, in_=rows[:].rearrange("p (s j d) -> p s j d", s=CHUNK_SLOTS, d=HD))
+
+                    if n in TENSOR_ADDS:
+                        base = sums[ch, half][:, part * PAIR_TILES * HD : (part + 1) * PAIR_TILES * HD].unsqueeze(2).to_broadcast([P, PAIR_TILES * HD, 2])
+                        waiting[n] = (((identity, base), (minus, pair[:])), CHUNK_SLOTS, dest)
+                        continue
+                    rows = work.tile([P, BANK], F32, tag="rows")
+                    out, base, minuend = pair_views(rows, part, sums[ch, half], pair)
+                    add(out=out, in0=base, in1=minuend, op=SUB)
+                    dest(rows)
+                elif kind == "value":
                     rows = work.tile([P, BANK], F32, tag="rows")
                     nc.scalar.copy(out=rows[:], in_=accs[n][:])
-                    dest = v_view[:, g, tiles, :]
+                    nc.sync.dma_start(out=v_view[:, g, tiles, :], in_=rows[:].rearrange("p (j d) -> p j d", d=HD))
                 else:
                     both = work.tile([P, 2, BANK], F32, tag="both")
-                    if place == KEY:
+                    if kind == "key":
                         positions = BANK_TILES // 2
                         products(both, accs[n], k_table[g], half * positions, positions, 2)
-                        dest = k_view[:, g, tiles, :]
+                        view = k_view[:, g, tiles, :]
                     else:
                         positions = 1
                         products(both, accs[n], q_table[g], place, positions, BANK_TILES)
-                        dest = q_view[:, g * QPK + place, tiles, :]
-                    rotated += 1
-                    if n == len(banks) - 1:
-                        rows = add_halves(nc.vector.tensor_tensor, both, positions, BANK_TILES // positions)
-                    elif place < QPK and rotated % TENSOR_ADDS_EVERY == 0 and n + TENSOR_ADDS_END < len(banks):
-                        waiting[n] = (both, dest)
+                        view = q_view[:, g * QPK + place, tiles, :]
+
+                    def dest(rows, view=view):
+                        nc.sync.dma_start(out=view, in_=rows[:].rearrange("p (j d) -> p j d", d=HD))
+
+                    if n in TENSOR_ADDS:
+                        waiting[n] = (((identity, both[:, 0, :]), (identity, both[:, 1, :])), positions, dest)
                         continue
-                    else:
-                        rows = add_halves(nc.gpsimd.tensor_tensor, both, positions, BANK_TILES // positions)
-                nc.sync.dma_start(out=dest, in_=rows[:].rearrange("p (j d) -> p j d", d=HD))
+                    dest(add_halves(add, both, positions, BANK_TILES // positions))

@@ -39,12 +39,13 @@ CHUNK_COLS = CHUNK_SLOTS * HD
 PAIR_TILES = 2
 QUANTISED_TOGETHER = ((0,), (1,), (2,), (3,), (4,), (5,))
 SPLIT = (1,)
-UNITS = (("split", 1), ("key", 4), ("query", 6), ("query", 7), ("value", 5), ("query", 8), ("query", 9), ("value", 11), ("key", 10))
-TENSOR_ADDS = (6, 9,)
-VECTOR_ADDS = ()
-LEAD_REGROUP = 8
-LEAD_MULTIPLY = 3
-TENSOR_ADD_LAG = 2
+UNITS = (("split", 1), ("key", 4), ("query", 6), ("query", 7), ("value", 5), ("key", 10), ("value", 11), ("query", 8), ("query", 9))
+TENSOR_ADDS = (5, 18)
+VECTOR_ADDS = (16,)
+LEAD_TABLE = 9
+LEAD_REGROUP = 12
+LEAD_MULTIPLY = 6
+TENSOR_ADD_LAG = 1
 
 
 def tile_causalselfattentiongqa_pa_kernel(tc, x, freqs_cis, W_attn, out_0, out_1, out_2):
@@ -125,10 +126,11 @@ def tile_causalselfattentiongqa_pa_kernel(tc, x, freqs_cis, W_attn, out_0, out_1
         def load_k_table(g):
             nc.sync.dma_start(out=k_table[g][:, 0, :, :], in_=k_freqs[:, g, :, :])
 
-        load_q_table(0)
+        load_w_pass(0, 0)
         load_x(0)
-        load_w(0)
+        load_w_pass(0, 1)
         load_x(1)
+        load_q_table(0)
         load_x(2)
         load_x(3)
         load_x(4)
@@ -136,13 +138,13 @@ def tile_causalselfattentiongqa_pa_kernel(tc, x, freqs_cis, W_attn, out_0, out_1
         load_x(6)
         load_x(7)
         load_w(1)
-        later_loads = ((load_w, 2), (load_k_table, 0), (load_w, 3), (load_q_table, 1), (load_k_table, 1), (load_w, 4), (load_w, 5),)
+        later_loads = ((load_w, 2), (load_k_table, 0), (load_w, 3), (load_q_table, 1), (load_w, 5), (load_k_table, 1), (load_w, 4),)
 
         def mix_table(ch):
             g, place = divmod(ch * CHUNK_SLOTS, GROUP_SLOTS)
             loaded = q_table[g][:, 0, place : place + CHUNK_SLOTS, :].rearrange("p r (f e) -> p (r f) e", e=2)
-            nc.gpsimd.tensor_tensor(out=q_mixed[ch][:, 0, :], in0=loaded[:, :, 0], in1=loaded[:, :, 1], op=ADD)
-            nc.gpsimd.tensor_tensor(out=q_mixed[ch][:, 1, :], in0=loaded[:, :, 0], in1=loaded[:, :, 1], op=SUB)
+            nc.vector.tensor_tensor(out=q_mixed[ch][:, 0, :], in0=loaded[:, :, 0], in1=loaded[:, :, 1], op=ADD)
+            nc.vector.tensor_tensor(out=q_mixed[ch][:, 1, :], in0=loaded[:, :, 0], in1=loaded[:, :, 1], op=SUB)
 
         def turn_table(table):
             loaded = table[:, 0, :, :].rearrange("p r (f e) -> p r f e", e=2)
@@ -289,7 +291,12 @@ def tile_causalselfattentiongqa_pa_kernel(tc, x, freqs_cis, W_attn, out_0, out_1
                 if ch not in regrouped:
                     regrouped.add(ch)
                     regroup_w(nc.scalar.copy, ch)
-                g = ch * CHUNK_SLOTS // GROUP_SLOTS
+
+            def turn_for(n):
+                if n >= len(banks):
+                    return
+                kind = banks[n][0]
+                g = chunk_of(n) * CHUNK_SLOTS // GROUP_SLOTS
                 if kind == "key" and ("k", g) not in tables:
                     tables.add(("k", g))
                     turn_table(k_table[g])
@@ -301,6 +308,8 @@ def tile_causalselfattentiongqa_pa_kernel(tc, x, freqs_cis, W_attn, out_0, out_1
                 if ch not in quantised:
                     for other in w_sets[ch][0]:
                         quantised.add(other)
+                        if other in SPLIT:
+                            mix_table(other)
                     quantise_w(ch)
 
             def quantise_next():
@@ -350,10 +359,9 @@ def tile_causalselfattentiongqa_pa_kernel(tc, x, freqs_cis, W_attn, out_0, out_1
             G = nc.gpsimd.tensor_tensor
             V = nc.vector.tensor_tensor
             W0 = (slice(0, 2 * HD),)
-            mix_table(1)
-            turn_table(q_table[0])
             turn_x(0)
             turn_x(1)
+            turn_table(q_table[0])
             regroup_w(nc.vector.tensor_copy, 0)
             quantise_x((0,))
             quantise_w(0)
@@ -441,6 +449,8 @@ def tile_causalselfattentiongqa_pa_kernel(tc, x, freqs_cis, W_attn, out_0, out_1
                     nc.scalar.copy(out=rows[:].rearrange("p (a b d) -> p b a d", a=order, d=HD), in_=total[:].rearrange("p (b a d) -> p b a d", a=order, d=HD))
                     dest(rows)
                 regroup_for(n + LEAD_REGROUP)
+                for ahead in range(LEAD_TABLE + 1):
+                    turn_for(n + ahead)
                 for ahead in range(1, LEAD_MULTIPLY + 1):
                     multiply_next(n + ahead)
                 if n - TENSOR_ADD_LAG in waiting:

@@ -39,11 +39,11 @@ CHUNK_COLS = CHUNK_SLOTS * HD
 PAIR_TILES = 2
 QUANTISED_TOGETHER = ((0,), (1,), (2,), (3,), (4,), (5,))
 SPLIT = (1,)
-UNITS = (("split", 1), ("key", 4), ("query", 6), ("query", 7), ("value", 5), ("key", 10), ("value", 11), ("query", 8), ("query", 9))
-TENSOR_ADDS = (5, 18)
-VECTOR_ADDS = (16,)
-LEAD_TABLE = 9
-LEAD_REGROUP = 12
+UNITS = (("split", 1), ("key", 4), ("query", 8), ("query", 9), ("value", 11), ("value", 5), ("key", 10), ("query", 6), ("query", 7))
+TENSOR_ADDS = (6, 18)
+VECTOR_ADDS = ()
+LEAD_TABLE = 11
+LEAD_REGROUP = 14
 LEAD_MULTIPLY = 6
 TENSOR_ADD_LAG = 1
 
@@ -138,7 +138,13 @@ def tile_causalselfattentiongqa_pa_kernel(tc, x, freqs_cis, W_attn, out_0, out_1
         load_x(6)
         load_x(7)
         load_w(1)
-        later_loads = ((load_w, 2), (load_k_table, 0), (load_w, 3), (load_q_table, 1), (load_w, 5), (load_k_table, 1), (load_w, 4),)
+        later_loads = ((load_w, 2), (load_k_table, 0), (load_w, 4), (load_q_table, 1), (load_w, 5), (load_k_table, 1), (load_w, 3),)
+
+        def turn_first():
+            loaded = q_table[0][:, 0, :CHUNK_SLOTS, :].rearrange("p r (f e) -> p r f e", e=2)
+            turned = q_table[0][:, 1, :CHUNK_SLOTS, :].rearrange("p r (f e) -> p r f e", e=2)
+            nc.vector.tensor_scalar(out=turned[:, :, :, 0], in0=loaded[:, :, :, 1], scalar1=-1.0, scalar2=None, op0=MULT)
+            nc.vector.tensor_copy(out=turned[:, :, :, 1], in_=loaded[:, :, :, 0])
 
         def mix_table(ch):
             g, place = divmod(ch * CHUNK_SLOTS, GROUP_SLOTS)
@@ -308,8 +314,6 @@ def tile_causalselfattentiongqa_pa_kernel(tc, x, freqs_cis, W_attn, out_0, out_1
                 if ch not in quantised:
                     for other in w_sets[ch][0]:
                         quantised.add(other)
-                        if other in SPLIT:
-                            mix_table(other)
                     quantise_w(ch)
 
             def quantise_next():
@@ -361,42 +365,44 @@ def tile_causalselfattentiongqa_pa_kernel(tc, x, freqs_cis, W_attn, out_0, out_1
             W0 = (slice(0, 2 * HD),)
             turn_x(0)
             turn_x(1)
-            turn_table(q_table[0])
+            turn_x(2)
             regroup_w(nc.vector.tensor_copy, 0)
             quantise_x((0,))
             quantise_w(0)
-            turn_x(2)
-            turn_x(3)
+            turn_first()
+            mix_table(1)
             quantise_x((1,))
-            a = multiply_wide(0, W0, (0,))
-            r = rotate(0, a, (0,), G)
+            m = multiply_wide(0, W0, (0,))
+            r = rotate(0, m, (0,), G)
             later(0, 2)
             store(r)
+            turn_x(3)
             turn_x(4)
             turn_x(5)
             quantise_x((2, 3))
-            a = multiply_wide(0, W0, (1,))
-            r = rotate(0, a, (1,), G)
+            m = multiply_wide(0, W0, (1,))
+            r = rotate(0, m, (1,), G)
             later(2, 4)
             store(r)
             turn_x(6)
             turn_x(7)
             quantise_x((4, 5))
-            a = multiply_wide(0, W0, (2, 3))
+            m = multiply_wide(0, W0, (2, 3))
             regroup_first(LEAD_REGROUP - 2)
-            r = rotate(0, a, (2, 3), G)
+            r = rotate(0, m, (2, 3), G)
             later(4, 6)
             store(r)
             quantise_x((6, 7))
-            a = multiply_wide(0, W0, (4, 5))
+            m = multiply_wide(0, W0, (4, 5))
             regroup_first(LEAD_REGROUP - 1)
-            r = rotate(0, a, (4, 5), G)
+            r = rotate(0, m, (4, 5), G)
             later(6, 7)
             store(r)
-            a = multiply_wide(0, W0, (6, 7))
+            m = multiply_wide(0, W0, (6, 7))
             regroup_first(LEAD_REGROUP)
             multiply_next(0)
-            r = rotate(0, a, (6, 7), G)
+            r = rotate(0, m, (6, 7), G)
+            later(7, 7)
             store(r)
 
             def sum_product(acc, cos):

@@ -39,11 +39,11 @@ CHUNK_COLS = CHUNK_SLOTS * HD
 PAIR_TILES = 2
 QUANTISED_TOGETHER = ((0,), (1,), (2,), (3,), (4,), (5,))
 SPLIT = (1,)
-UNITS = (("split", 1), ("key", 4), ("query", 8), ("query", 9), ("value", 11), ("value", 5), ("key", 10), ("query", 6), ("query", 7))
-TENSOR_ADDS = (6, 18)
-VECTOR_ADDS = ()
-LEAD_TABLE = 11
-LEAD_REGROUP = 14
+UNITS = (("query", 8), ("query", 9), ("split", 1), ("value", 5), ("key", 10), ("key", 4), ("value", 11), ("query", 6), ("query", 7))
+TENSOR_ADDS = (12, 18)
+VECTOR_ADDS = (20,)
+LEAD_TABLE = 2
+LEAD_REGROUP = 8
 LEAD_MULTIPLY = 6
 TENSOR_ADD_LAG = 1
 
@@ -138,7 +138,7 @@ def tile_causalselfattentiongqa_pa_kernel(tc, x, freqs_cis, W_attn, out_0, out_1
         load_x(6)
         load_x(7)
         load_w(1)
-        later_loads = ((load_w, 2), (load_k_table, 0), (load_w, 4), (load_q_table, 1), (load_w, 5), (load_k_table, 1), (load_w, 3),)
+        later_loads = ((load_w, 4), (load_q_table, 1), (load_w, 2), (load_w, 5), (load_k_table, 1), (load_k_table, 0), (load_w, 3),)
 
         def turn_first():
             loaded = q_table[0][:, 0, :CHUNK_SLOTS, :].rearrange("p r (f e) -> p r f e", e=2)
@@ -489,6 +489,20 @@ def tile_causalselfattentiongqa_pa_kernel(tc, x, freqs_cis, W_attn, out_0, out_1
                     rows = work.tile([P, BANK], F32, tag="rows")
                     nc.scalar.copy(out=rows[:], in_=accs[n][:])
                     nc.sync.dma_start(out=v_view[:, g, tiles, :], in_=rows[:].rearrange("p (j d) -> p j d", d=HD))
+                elif n == len(banks) - 1:
+                    width = PAIR_TILES * HD
+                    halves = []
+                    for part in range(2):
+                        both = work.tile([P, 2, BANK], F32, tag="both")
+                        products(both, accs[n][:, part * width : (part + 1) * width], q_table[g], place, 1, PAIR_TILES)
+                        halves.append(both)
+                    for part, combine in enumerate((G, V)):
+                        rows = add_halves(combine, halves[part], 1, PAIR_TILES)
+                        first = half * BANK_TILES + part * PAIR_TILES
+                        nc.sync.dma_start(
+                            out=q_view[:, g * QPK + place, first : first + PAIR_TILES, :],
+                            in_=rows[:, :width].rearrange("p (j d) -> p j d", d=HD),
+                        )
                 else:
                     both = work.tile([P, 2, BANK], F32, tag="both")
                     if kind == "key":

@@ -39,13 +39,13 @@ CHUNK_COLS = CHUNK_SLOTS * HD
 PAIR_TILES = 2
 QUANTISED_TOGETHER = ((0,), (1,), (2,), (3,), (4,), (5,))
 SPLIT = (1,)
-UNITS = (("query", 8), ("query", 9), ("split", 1), ("value", 5), ("key", 10), ("key", 4), ("value", 11), ("query", 6), ("query", 7))
-TENSOR_ADDS = (12, 18)
-VECTOR_ADDS = (20,)
-LEAD_TABLE = 2
-LEAD_REGROUP = 8
-LEAD_MULTIPLY = 6
-TENSOR_ADD_LAG = 1
+UNITS = (("split", 1), ("query", 8), ("query", 9), ("key", 4), ("value", 11), ("key", 10), ("value", 5), ("query", 6), ("query", 7))
+TENSOR_ADDS = (4, 18)
+VECTOR_ADDS = (17, 20)
+LEAD_TABLE = 8
+LEAD_REGROUP = 11
+LEAD_MULTIPLY = 4
+TENSOR_ADD_LAG = 2
 
 
 def tile_causalselfattentiongqa_pa_kernel(tc, x, freqs_cis, W_attn, out_0, out_1, out_2):
@@ -138,7 +138,7 @@ def tile_causalselfattentiongqa_pa_kernel(tc, x, freqs_cis, W_attn, out_0, out_1
         load_x(6)
         load_x(7)
         load_w(1)
-        later_loads = ((load_w, 4), (load_q_table, 1), (load_w, 2), (load_w, 5), (load_k_table, 1), (load_k_table, 0), (load_w, 3),)
+        later_loads = ((load_w, 4), (load_q_table, 1), (load_w, 2), (load_k_table, 0), (load_w, 5), (load_k_table, 1), (load_w, 3),)
 
         def turn_first():
             loaded = q_table[0][:, 0, :CHUNK_SLOTS, :].rearrange("p r (f e) -> p r f e", e=2)
@@ -365,18 +365,18 @@ def tile_causalselfattentiongqa_pa_kernel(tc, x, freqs_cis, W_attn, out_0, out_1
             W0 = (slice(0, 2 * HD),)
             turn_x(0)
             turn_x(1)
-            turn_x(2)
             regroup_w(nc.vector.tensor_copy, 0)
             quantise_x((0,))
             quantise_w(0)
             turn_first()
             mix_table(1)
+            turn_x(2)
+            turn_x(3)
             quantise_x((1,))
             m = multiply_wide(0, W0, (0,))
             r = rotate(0, m, (0,), G)
             later(0, 2)
             store(r)
-            turn_x(3)
             turn_x(4)
             turn_x(5)
             quantise_x((2, 3))

@@ -38,13 +38,13 @@ CHUNKS = GROUPS * GROUP_SLOTS // CHUNK_SLOTS
 CHUNK_COLS = CHUNK_SLOTS * HD
 PAIR_TILES = 2
 QUANTISED_TOGETHER = ((0,), (1,), (2,), (3,), (4,), (5,))
-SPLIT = (1,)
-UNITS = (("split", 1), ("query", 8), ("query", 9), ("key", 4), ("value", 11), ("key", 10), ("value", 5), ("query", 6), ("query", 7))
-TENSOR_ADDS = (4, 18)
-VECTOR_ADDS = (17, 20)
-LEAD_TABLE = 8
-LEAD_REGROUP = 11
-LEAD_MULTIPLY = 4
+SPLIT = ()
+UNITS = (("duo", 1), ("value", 11), ("key", 10), ("key", 4), ("duo", 3), ("value", 5), ("duo", 4))
+TENSOR_ADDS = (2, 10, 16)
+VECTOR_ADDS = (18,)
+LEAD_TABLE = 6
+LEAD_REGROUP = 9
+LEAD_MULTIPLY = 3
 TENSOR_ADD_LAG = 2
 
 
@@ -138,11 +138,11 @@ def tile_causalselfattentiongqa_pa_kernel(tc, x, freqs_cis, W_attn, out_0, out_1
         load_x(6)
         load_x(7)
         load_w(1)
-        later_loads = ((load_w, 4), (load_q_table, 1), (load_w, 2), (load_k_table, 0), (load_w, 5), (load_k_table, 1), (load_w, 3),)
+        later_loads = ((load_w, 5), (load_k_table, 1), (load_w, 2), (load_k_table, 0), (load_w, 3), (load_q_table, 1), (load_w, 4),)
 
         def turn_first():
-            loaded = q_table[0][:, 0, :CHUNK_SLOTS, :].rearrange("p r (f e) -> p r f e", e=2)
-            turned = q_table[0][:, 1, :CHUNK_SLOTS, :].rearrange("p r (f e) -> p r f e", e=2)
+            loaded = q_table[0][:, 0, : (CHUNK_SLOTS if 1 in SPLIT else QPK), :].rearrange("p r (f e) -> p r f e", e=2)
+            turned = q_table[0][:, 1, : (CHUNK_SLOTS if 1 in SPLIT else QPK), :].rearrange("p r (f e) -> p r f e", e=2)
             nc.vector.tensor_scalar(out=turned[:, :, :, 0], in0=loaded[:, :, :, 1], scalar1=-1.0, scalar2=None, op0=MULT)
             nc.vector.tensor_copy(out=turned[:, :, :, 1], in_=loaded[:, :, :, 0])
 
@@ -278,6 +278,9 @@ def tile_causalselfattentiongqa_pa_kernel(tc, x, freqs_cis, W_attn, out_0, out_1
                         banks.append(("sum", what, half, 0))
                         banks.append(("pair", what, half, 0))
                         banks.append(("pair", what, half, 1))
+                    elif kind == "duo":
+                        banks.append(("duo", what, half, 0))
+                        banks.append(("duo", what, half, 1))
                     else:
                         banks.append((kind, what, half, 0))
             regrouped = set()
@@ -287,7 +290,7 @@ def tile_causalselfattentiongqa_pa_kernel(tc, x, freqs_cis, W_attn, out_0, out_1
 
             def chunk_of(n):
                 kind, what = banks[n][:2]
-                return what if kind in ("sum", "pair") else what // CHUNK_SLOTS
+                return what if kind in ("sum", "pair", "duo") else what // CHUNK_SLOTS
 
             def regroup_for(n):
                 if n >= len(banks):
@@ -306,7 +309,7 @@ def tile_causalselfattentiongqa_pa_kernel(tc, x, freqs_cis, W_attn, out_0, out_1
                 if kind == "key" and ("k", g) not in tables:
                     tables.add(("k", g))
                     turn_table(k_table[g])
-                if kind == "query" and g > 0 and ("q", g) not in tables:
+                if kind == "duo" and g > 0 and ("q", g) not in tables:
                     tables.add(("q", g))
                     turn_table(q_table[g])
 
@@ -314,6 +317,8 @@ def tile_causalselfattentiongqa_pa_kernel(tc, x, freqs_cis, W_attn, out_0, out_1
                 if ch not in quantised:
                     for other in w_sets[ch][0]:
                         quantised.add(other)
+                        if other in SPLIT and other != 1:
+                            mix_table(other)
                     quantise_w(ch)
 
             def quantise_next():
@@ -330,7 +335,7 @@ def tile_causalselfattentiongqa_pa_kernel(tc, x, freqs_cis, W_attn, out_0, out_1
                 first = half * BANK_TILES
                 if kind == "sum":
                     accs[n] = multiply_wide(what, (slice(0, HD), slice(HD, 2 * HD)), range(first, first + BANK_TILES))
-                elif kind == "pair":
+                elif kind in ("pair", "duo"):
                     first += part * PAIR_TILES
                     accs[n] = multiply_wide(what, (slice(0, 2 * HD),), range(first, first + PAIR_TILES))
                 elif kind == "key":
@@ -369,7 +374,9 @@ def tile_causalselfattentiongqa_pa_kernel(tc, x, freqs_cis, W_attn, out_0, out_1
             quantise_x((0,))
             quantise_w(0)
             turn_first()
-            mix_table(1)
+            for c in SPLIT:
+                if c == 1:
+                    mix_table(c)
             turn_x(2)
             turn_x(3)
             quantise_x((1,))
@@ -463,7 +470,7 @@ def tile_causalselfattentiongqa_pa_kernel(tc, x, freqs_cis, W_attn, out_0, out_1
                     terms, order, dest = waiting[n - TENSOR_ADD_LAG]
                     totals[n] = (add_in_psum(terms), order, dest)
                 ch = chunk_of(n)
-                g, place = divmod(ch * CHUNK_SLOTS if kind in ("sum", "pair") else what, GROUP_SLOTS)
+                g, place = divmod(ch * CHUNK_SLOTS if kind in ("sum", "pair", "duo") else what, GROUP_SLOTS)
                 tiles = slice(half * BANK_TILES, (half + 1) * BANK_TILES)
                 add = V if n == len(banks) - 1 or n in VECTOR_ADDS else G
                 if kind == "sum":
@@ -490,32 +497,36 @@ def tile_causalselfattentiongqa_pa_kernel(tc, x, freqs_cis, W_attn, out_0, out_1
                     nc.scalar.copy(out=rows[:], in_=accs[n][:])
                     nc.sync.dma_start(out=v_view[:, g, tiles, :], in_=rows[:].rearrange("p (j d) -> p j d", d=HD))
                 elif n == len(banks) - 1:
-                    width = PAIR_TILES * HD
+                    width = CHUNK_SLOTS * HD
                     halves = []
-                    for part in range(2):
+                    for j in range(PAIR_TILES):
                         both = work.tile([P, 2, BANK], F32, tag="both")
-                        products(both, accs[n][:, part * width : (part + 1) * width], q_table[g], place, 1, PAIR_TILES)
+                        products(both, accs[n][:, j * width : (j + 1) * width], q_table[g], place, CHUNK_SLOTS, 1)
                         halves.append(both)
-                    for part, combine in enumerate((G, V)):
-                        rows = add_halves(combine, halves[part], 1, PAIR_TILES)
-                        first = half * BANK_TILES + part * PAIR_TILES
+                    for j, combine in enumerate((G, V)):
+                        rows = add_halves(combine, halves[j], CHUNK_SLOTS, 1)
+                        first = half * BANK_TILES + part * PAIR_TILES + j
                         nc.sync.dma_start(
-                            out=q_view[:, g * QPK + place, first : first + PAIR_TILES, :],
-                            in_=rows[:, :width].rearrange("p (j d) -> p j d", d=HD),
+                            out=q_view[:, g * QPK + place : g * QPK + place + CHUNK_SLOTS, first : first + 1, :],
+                            in_=rows[:, :width].rearrange("p (a j d) -> p a j d", a=CHUNK_SLOTS, d=HD),
                         )
                 else:
                     both = work.tile([P, 2, BANK], F32, tag="both")
+                    positions = 2
                     if kind == "key":
-                        positions = BANK_TILES // 2
                         products(both, accs[n], k_table[g], half * positions, positions, 2)
                         view = k_view[:, g, tiles, :]
-                    else:
-                        positions = 1
-                        products(both, accs[n], q_table[g], place, positions, BANK_TILES)
-                        view = q_view[:, g * QPK + place, tiles, :]
 
-                    def dest(rows, view=view):
-                        nc.sync.dma_start(out=view, in_=rows[:].rearrange("p (j d) -> p j d", d=HD))
+                        def dest(rows, view=view):
+                            nc.sync.dma_start(out=view, in_=rows[:].rearrange("p (j d) -> p j d", d=HD))
+
+                    else:
+                        products(both, accs[n], q_table[g], place, positions, 2)
+                        first = half * BANK_TILES + part * PAIR_TILES
+                        view = q_view[:, g * QPK + place : g * QPK + place + CHUNK_SLOTS, first : first + PAIR_TILES, :]
+
+                        def dest(rows, view=view):
+                            nc.sync.dma_start(out=view, in_=rows[:].rearrange("p (a j d) -> p a j d", a=CHUNK_SLOTS, d=HD))
 
                     if n in TENSOR_ADDS:
                         waiting[n] = (((identity, both[:, 0, :]), (identity, both[:, 1, :])), positions, dest)

from contextlib import ExitStack

import concourse.mybir as mybir
from concourse.masks import make_identity

BF16 = mybir.dt.bfloat16
F32 = mybir.dt.float32
U32 = mybir.dt.uint32
U8 = mybir.dt.uint8
FP8X4 = mybir.dt.float8_e4m3fn_x4
MULT = mybir.AluOpType.mult
ADD = mybir.AluOpType.add
SUB = mybir.AluOpType.subtract
COPY = mybir.ActivationFunctionType.Copy

P = 128
PACK = 4
K_PASS = P * PACK
TOKENS = 1024
K = 1024
PASSES = K // K_PASS
TILES = TOKENS // P
HD = 128
HALF = HD // 2
GROUPS = 2
QPK = 4
GROUP_SLOTS = QPK + 2
KEY = QPK
VALUE = QPK + 1
BANK_TILES = 4
BANK = BANK_TILES * HD
KEY_ROWS = TILES // 2

FLOPS = 2 * TOKENS * K * GROUPS * GROUP_SLOTS * HD

CHUNK_SLOTS = 2
CHUNKS = GROUPS * GROUP_SLOTS // CHUNK_SLOTS
CHUNK_COLS = CHUNK_SLOTS * HD
PAIR_TILES = 2
QUANTISED_TOGETHER = ((0,), (1,), (2,), (3,), (4,), (5,))
SPLIT = ()
UNITS = (("duo", 1), ("value", 11), ("key", 10), ("key", 4), ("duo", 3), ("value", 5), ("duo", 4))
TENSOR_ADDS = (2, 10, 16)
VECTOR_ADDS = (18,)
LEAD_TABLE = 6
LEAD_REGROUP = 9
LEAD_MULTIPLY = 3
TENSOR_ADD_LAG = 2


def tile_causalselfattentiongqa_pa_kernel(tc, x, freqs_cis, W_attn, out_0, out_1, out_2):
    nc = tc.nc
    with ExitStack() as ctx:
        keep = ctx.enter_context(tc.tile_pool(name="keep", bufs=1))
        work = ctx.enter_context(tc.tile_pool(name="work", bufs=8))
        psum = ctx.enter_context(tc.psum_pool(name="psum", bufs=8))

        x_view = x.flatten_outer_dims().rearrange("(i j) k -> i (j k)", j=TILES)
        w_view = W_attn.rearrange("(c p t) n -> p c t n", c=PASSES, t=PACK)
        q_view = out_0.rearrange("o n h d -> (o n h) d").rearrange(
            "(a i j) d -> i a j d", a=GROUPS * QPK, j=TILES
        )
        k_view = out_1.rearrange("o n h d -> (o n h) d").rearrange(
            "(g i j) d -> i g j d", g=GROUPS, j=TILES
        )
        v_view = out_2.rearrange("o n h d -> (o n h) d").rearrange(
            "(g i j) d -> i g j d", g=GROUPS, j=TILES
        )
        q_freqs = freqs_cis.rearrange("(a i) f e -> i a (f e)", a=GROUPS * QPK)
        k_freqs = freqs_cis.rearrange("(g i r) f e -> i g r (f e)", g=GROUPS, r=KEY_ROWS)

        x_sb = keep.tile([P, TILES * K], BF16)
        x_grouped = keep.tile([P, TILES * K], BF16, align_bytes=64)
        x_codes = keep.tile([P, TILES * PASSES * P], U32, align_bytes=64)
        x_scales = keep.tile([P, TILES * PASSES * P], U8, align_bytes=64)
        w_raw = []
        w_grouped = []
        w_codes = []
        w_scales = []
        for ch in range(CHUNKS):
            w_raw.append(keep.tile([P, PASSES, PACK, CHUNK_COLS], BF16, name="w_raw%d" % ch))
        w_grouped = {}
        w_codes = {}
        w_scales = {}
        w_sets = {}
        for chunks in QUANTISED_TOGETHER:
            grouped = keep.tile([P, len(chunks), PASSES, CHUNK_COLS, PACK], BF16, name="w_grouped%d" % chunks[0], align_bytes=64)
            codes = keep.tile([P, len(chunks), PASSES, CHUNK_COLS], U32, name="w_codes%d" % chunks[0], align_bytes=64)
            scales = keep.tile([P, len(chunks), PASSES, CHUNK_COLS], U8, name="w_scales%d" % chunks[0], align_bytes=64)
            for n, ch in enumerate(chunks):
                w_grouped[ch] = grouped[:, n]
                w_codes[ch] = codes[:, n]
                w_scales[ch] = scales[:, n]
                w_sets[ch] = (chunks, grouped, codes, scales)
        q_table = []
        k_table = []
        for g in range(GROUPS):
            q_table.append(keep.tile([P, 2, QPK, HD], BF16, name="q_table%d" % g))
            k_table.append(keep.tile([P, 2, KEY_ROWS, HD], BF16, name="k_table%d" % g))
        q_mixed = {}
        for ch in SPLIT:
            q_mixed[ch] = keep.tile([P, 2, CHUNK_SLOTS * HALF], F32, name="q_mixed%d" % ch)
        identity = keep.tile([P, P], F32)
        minus = keep.tile([P, P], F32)

        make_identity(nc, identity[:])
        nc.scalar.activation(out=minus[:], in_=identity[:], func=COPY, scale=-1.0)

        def load_x(j):
            cols = slice(j * K, (j + 1) * K)
            nc.sync.dma_start(out=x_sb[:, cols], in_=x_view[:, cols])

        def load_w(ch):
            for c in range(PASSES):
                nc.sync.dma_start(
                    out=w_raw[ch][:, c, :, :],
                    in_=w_view[:, c, :, ch * CHUNK_COLS : (ch + 1) * CHUNK_COLS],
                )

        def load_w_pass(ch, c):
            nc.sync.dma_start(out=w_raw[ch][:, c, :, :], in_=w_view[:, c, :, ch * CHUNK_COLS : (ch + 1) * CHUNK_COLS])

        def load_q_table(g):
            nc.sync.dma_start(out=q_table[g][:, 0, :, :], in_=q_freqs[:, g * QPK : (g + 1) * QPK, :])

        def load_k_table(g):
            nc.sync.dma_start(out=k_table[g][:, 0, :, :], in_=k_freqs[:, g, :, :])

        load_w_pass(0, 0)
        load_x(0)
        load_w_pass(0, 1)
        load_x(1)
        load_q_table(0)
        load_x(2)
        load_x(3)
        load_x(4)
        load_x(5)
        load_x(6)
        load_x(7)
        load_w(1)
        later_loads = ((load_w, 5), (load_k_table, 1), (load_w, 2), (load_k_table, 0), (load_w, 3), (load_q_table, 1), (load_w, 4),)

        def turn_first():
            loaded = q_table[0][:, 0, : (CHUNK_SLOTS if 1 in SPLIT else QPK), :].rearrange("p r (f e) -> p r f e", e=2)
            turned = q_table[0][:, 1, : (CHUNK_SLOTS if 1 in SPLIT else QPK), :].rearrange("p r (f e) -> p r f e", e=2)
            nc.vector.tensor_scalar(out=turned[:, :, :, 0], in0=loaded[:, :, :, 1], scalar1=-1.0, scalar2=None, op0=MULT)
            nc.vector.tensor_copy(out=turned[:, :, :, 1], in_=loaded[:, :, :, 0])

        def mix_table(ch):
            g, place = divmod(ch * CHUNK_SLOTS, GROUP_SLOTS)
            loaded = q_table[g][:, 0, place : place + CHUNK_SLOTS, :].rearrange("p r (f e) -> p (r f) e", e=2)
            nc.vector.tensor_tensor(out=q_mixed[ch][:, 0, :], in0=loaded[:, :, 0], in1=loaded[:, :, 1], op=ADD)
            nc.vector.tensor_tensor(out=q_mixed[ch][:, 1, :], in0=loaded[:, :, 0], in1=loaded[:, :, 1], op=SUB)

        def turn_table(table):
            loaded = table[:, 0, :, :].rearrange("p r (f e) -> p r f e", e=2)
            turned = table[:, 1, :, :].rearrange("p r (f e) -> p r f e", e=2)
            nc.scalar.activation(out=turned[:, :, :, 0], in_=loaded[:, :, :, 1], func=COPY, scale=-1.0)
            nc.scalar.copy(out=turned[:, :, :, 1], in_=loaded[:, :, :, 0])

        def regroup_pass(copy, ch, c):
            if ch in SPLIT:
                for e in range(2):
                    copy(
                        out=w_grouped[ch][:, c, e * HD : (e + 1) * HD, :].rearrange("p (n i) t -> p n t i", i=4),
                        in_=w_raw[ch][:, c, :, :].rearrange("p t (n i e) -> p e n t i", i=4, e=2)[:, 1 - e],
                    )
            else:
                copy(
                    out=w_grouped[ch][:, c, :, :].rearrange("p (n i) t -> p n t i", i=4),
                    in_=w_raw[ch][:, c, :, :].rearrange("p t (n i) -> p n t i", i=4),
                )

        def regroup_w(copy, ch):
            for c in range(PASSES):
                regroup_pass(copy, ch, c)

        def quantise_w(ch):
            grouped, codes, scales = w_sets[ch][1:]
            nc.vector.quantize_mx(
                out=codes[:].rearrange("p h c n -> p (h c n)").bitcast(FP8X4),
                scales=scales[:].rearrange("p h c n -> p (h c n)"),
                in_=grouped[:].rearrange("p h c n t -> p (h c n t)"),
            )

        x_words = x_sb[:].bitcast(F32).rearrange(
            "i (j c p u) -> i j c u p", j=TILES, c=PASSES, u=2
        )

        def turn_x(j):
            turned = psum.tile([P, PASSES * 2, P], F32, tag="bank")
            for c in range(PASSES):
                for u in range(2):
                    nc.tensor.transpose(turned[:, 2 * c + u, :], x_words[:, j, c, u, :], identity[:])
            cols = slice(j * K, (j + 1) * K)
            nc.scalar.copy(
                out=x_grouped[:, cols].bitcast(F32).rearrange("p (c i u) -> p c i u", c=PASSES, u=2),
                in_=turned[:].rearrange("p (c u) i -> p c i u", c=PASSES),
            )

        def quantise_x(tiles):
            first, after = tiles[0], tiles[-1] + 1
            words = slice(first * PASSES * P, after * PASSES * P)
            nc.vector.quantize_mx(
                out=x_codes[:, words].bitcast(FP8X4),
                scales=x_scales[:, words],
                in_=x_grouped[:, first * K : after * K],
            )

        def multiply(pieces):
            acc = psum.tile([P, BANK], F32, tag="bank")
            for n, (slot, j) in enumerate(pieces):
                ch, at = divmod(slot, CHUNK_SLOTS)
                cols = slice(at * HD, (at + 1) * HD)
                for c in range(PASSES):
                    tokens = slice((j * PASSES + c) * P, (j * PASSES + c + 1) * P)
                    nc.tensor.matmul_mx(
                        out=acc[:, n * HD : (n + 1) * HD],
                        lhsT=x_codes[:, tokens].bitcast(FP8X4),
                        lhsT_scale=x_scales[:, tokens],
                        rhs=w_codes[ch][:, c, cols].bitcast(FP8X4),
                        rhs_scale=w_scales[ch][:, c, cols],
                        start=(c == 0),
                        stop=(c == PASSES - 1),
                    )
            return acc

        def multiply_wide(ch, terms, tiles):
            acc = psum.tile([P, BANK], F32, tag="bank")
            width = terms[0].stop - terms[0].start
            for n, j in enumerate(tiles):
                passes = [(c, cols) for c in range(PASSES) for cols in terms]
                for m, (c, cols) in enumerate(passes):
                    tokens = slice((j * PASSES + c) * P, (j * PASSES + c + 1) * P)
                    nc.tensor.matmul_mx(
                        out=acc[:, n * width : (n + 1) * width],
                        lhsT=x_codes[:, tokens].bitcast(FP8X4),
                        lhsT_scale=x_scales[:, tokens],
                        rhs=w_codes[ch][:, c, cols].bitcast(FP8X4),
                        rhs_scale=w_scales[ch][:, c, cols],
                        start=(m == 0),
                        stop=(m == len(passes) - 1),
                    )
            return acc

        def products(both, acc, table, first, positions, repeats):
            width = repeats * positions * HD
            shape = [P, 2, repeats, positions * HALF, 2]
            nc.vector.tensor_tensor(
                out=both[:, :, :width].rearrange("p h (j q e) -> p h j q e", j=repeats, e=2),
                in0=acc[:, :width]
                .rearrange("p (j q h) -> p h j q", j=repeats, h=2)
                .unsqueeze(4)
                .to_broadcast(shape),
                in1=table[:, :, first : first + positions, :]
                .rearrange("p h r (f e) -> p h (r f) e", e=2)
                .unsqueeze(2)
                .to_broadcast(shape),
                op=MULT,
            )

        def add_halves(add, both, positions, repeats):
            width = repeats * positions * HD
            rows = work.tile([P, BANK], F32, tag="rows")
            add(
                out=rows[:, :width].rearrange("p (r j d) -> p j r d", r=positions, d=HD),
                in0=both[:, 0, :width].rearrange("p (j r d) -> p j r d", r=positions, d=HD),
                in1=both[:, 1, :width].rearrange("p (j r d) -> p j r d", r=positions, d=HD),
                op=ADD,
            )
            return rows

        with tc.manual_schedule():
            banks = []
            for kind, what in UNITS:
                for half in range(TILES // BANK_TILES):
                    if kind == "split":
                        banks.append(("sum", what, half, 0))
                        banks.append(("pair", what, half, 0))
                        banks.append(("pair", what, half, 1))
                    elif kind == "duo":
                        banks.append(("duo", what, half, 0))
                        banks.append(("duo", what, half, 1))
                    else:
                        banks.append((kind, what, half, 0))
            regrouped = set()
            quantised = set()
            tables = set()
            accs = {}

            def chunk_of(n):
                kind, what = banks[n][:2]
                return what if kind in ("sum", "pair", "duo") else what // CHUNK_SLOTS

            def regroup_for(n):
                if n >= len(banks):
                    return
                kind, what = banks[n][:2]
                ch = chunk_of(n)
                if ch not in regrouped:
                    regrouped.add(ch)
                    regroup_w(nc.scalar.copy, ch)

            def turn_for(n):
                if n >= len(banks):
                    return
                kind = banks[n][0]
                g = chunk_of(n) * CHUNK_SLOTS // GROUP_SLOTS
                if kind == "key" and ("k", g) not in tables:
                    tables.add(("k", g))
                    turn_table(k_table[g])
                if kind == "duo" and g > 0 and ("q", g) not in tables:
                    tables.add(("q", g))
                    turn_table(q_table[g])

            def quantise_for(ch):
                if ch not in quantised:
                    for other in w_sets[ch][0]:
                        quantised.add(other)
                        if other in SPLIT and other != 1:
                            mix_table(other)
                    quantise_w(ch)

            def quantise_next():
                for n in range(len(banks)):
                    if chunk_of(n) not in quantised:
                        quantise_for(chunk_of(n))
                        return

            def multiply_next(n):
                if n >= len(banks) or n in accs:
                    return
                kind, what, half, part = banks[n]
                quantise_for(chunk_of(n))
                first = half * BANK_TILES
                if kind == "sum":
                    accs[n] = multiply_wide(what, (slice(0, HD), slice(HD, 2 * HD)), range(first, first + BANK_TILES))
                elif kind in ("pair", "duo"):
                    first += part * PAIR_TILES
                    accs[n] = multiply_wide(what, (slice(0, 2 * HD),), range(first, first + PAIR_TILES))
                elif kind == "key":
                    accs[n] = multiply([(what, first + 2 * r + j) for j in range(2) for r in range(BANK_TILES // 2)])
                else:
                    accs[n] = multiply([(what, first + j) for j in range(BANK_TILES)])

            def rotate(ch, acc, group, add):
                both = work.tile([P, 2, BANK], F32, tag="both")
                products(both, acc, q_table[0], ch * CHUNK_SLOTS, CHUNK_SLOTS, len(group))
                rows = add_halves(add, both, CHUNK_SLOTS, len(group))
                return (ch, rows, group)

            def store(what):
                ch, rows, group = what
                width = CHUNK_SLOTS * len(group) * HD
                nc.sync.dma_start(
                    out=q_view[:, ch * CHUNK_SLOTS : (ch + 1) * CHUNK_SLOTS, group[0] : group[-1] + 1, :],
                    in_=rows[:, :width].rearrange("p (a j d) -> p a j d", a=CHUNK_SLOTS, d=HD),
                )

            def later(first, after):
                for load, what in later_loads[first:after]:
                    load(what)

            def regroup_first(count):
                for n in range(count):
                    regroup_for(n)

            G = nc.gpsimd.tensor_tensor
            V = nc.vector.tensor_tensor
            W0 = (slice(0, 2 * HD),)
            turn_x(0)
            turn_x(1)
            regroup_w(nc.vector.tensor_copy, 0)
            quantise_x((0,))
            quantise_w(0)
            turn_first()
            for c in SPLIT:
                if c == 1:
                    mix_table(c)
            turn_x(2)
            turn_x(3)
            quantise_x((1,))
            m = multiply_wide(0, W0, (0,))
            r = rotate(0, m, (0,), G)
            later(0, 2)
            store(r)
            turn_x(4)
            turn_x(5)
            quantise_x((2, 3))
            m = multiply_wide(0, W0, (1,))
            r = rotate(0, m, (1,), G)
            later(2, 4)
            store(r)
            turn_x(6)
            turn_x(7)
            quantise_x((4, 5))
            m = multiply_wide(0, W0, (2, 3))
            regroup_first(LEAD_REGROUP - 2)
            r = rotate(0, m, (2, 3), G)
            later(4, 6)
            store(r)
            quantise_x((6, 7))
            m = multiply_wide(0, W0, (4, 5))
            regroup_first(LEAD_REGROUP - 1)
            r = rotate(0, m, (4, 5), G)
            later(6, 7)
            store(r)
            m = multiply_wide(0, W0, (6, 7))
            regroup_first(LEAD_REGROUP)
            multiply_next(0)
            r = rotate(0, m, (6, 7), G)
            later(7, 7)
            store(r)

            def sum_product(acc, cos):
                prod = work.tile([P, BANK], F32, tag="sum", bufs=4)
                shape = [P, BANK_TILES, HD]
                nc.vector.tensor_tensor(
                    out=prod[:].rearrange("p (j q) -> p j q", q=HD),
                    in0=acc[:].rearrange("p (j q) -> p j q", q=HD),
                    in1=cos.unsqueeze(1).to_broadcast(shape),
                    op=MULT,
                )
                return prod

            def pair_product(acc, mixed):
                prod = work.tile([P, BANK], F32, tag="pair")
                shape = [P, PAIR_TILES, HD, 2]
                nc.vector.tensor_tensor(
                    out=prod[:].rearrange("p (j q e) -> p j q e", j=PAIR_TILES, e=2),
                    in0=acc[:].rearrange("p (j e q) -> p j q e", j=PAIR_TILES, e=2),
                    in1=mixed.rearrange("p e q -> p q e").unsqueeze(1).to_broadcast(shape),
                    op=MULT,
                )
                return prod

            def pair_views(rows, part, sums, pair):
                shape = [P, PAIR_TILES, CHUNK_SLOTS, HALF, 2]
                return (
                    rows[:].rearrange("p (s j f e) -> p j s f e", j=PAIR_TILES, f=HALF, e=2),
                    sums[:, part * PAIR_TILES * HD : (part + 1) * PAIR_TILES * HD]
                    .rearrange("p (j s f) -> p j s f", j=PAIR_TILES, s=CHUNK_SLOTS)
                    .unsqueeze(4)
                    .to_broadcast(shape),
                    pair[:].rearrange("p (j s f e) -> p j s f e", j=PAIR_TILES, s=CHUNK_SLOTS, e=2),
                )

            def add_in_psum(terms):
                total = psum.tile([P, BANK], F32, tag="bank")
                for n, (factor, term) in enumerate(terms):
                    nc.tensor.matmul(out=total[:], lhsT=factor[:], rhs=term, start=(n == 0), stop=(n == 1))
                return total

            waiting = {}
            totals = {}
            sums = {}
            split_rows = {}
            for n, (kind, what, half, part) in enumerate(banks):
                if n - 1 in totals:
                    total, order, dest = totals[n - 1]
                    rows = work.tile([P, BANK], F32, tag="rows")
                    nc.scalar.copy(out=rows[:].rearrange("p (a b d) -> p b a d", a=order, d=HD), in_=total[:].rearrange("p (b a d) -> p b a d", a=order, d=HD))
                    dest(rows)
                regroup_for(n + LEAD_REGROUP)
                for ahead in range(LEAD_TABLE + 1):
                    turn_for(n + ahead)
                for ahead in range(1, LEAD_MULTIPLY + 1):
                    multiply_next(n + ahead)
                if n - TENSOR_ADD_LAG in waiting:
                    terms, order, dest = waiting[n - TENSOR_ADD_LAG]
                    totals[n] = (add_in_psum(terms), order, dest)
                ch = chunk_of(n)
                g, place = divmod(ch * CHUNK_SLOTS if kind in ("sum", "pair", "duo") else what, GROUP_SLOTS)
                tiles = slice(half * BANK_TILES, (half + 1) * BANK_TILES)
                add = V if n == len(banks) - 1 or n in VECTOR_ADDS else G
                if kind == "sum":
                    cos = q_table[g][:, 0, place : place + CHUNK_SLOTS, :].rearrange("p r (f e) -> p (r f) e", e=2)[:, :, 0]
                    sums[ch, half] = sum_product(accs[n], cos)
                elif kind == "pair":
                    pair = pair_product(accs[n], q_mixed[ch][:])
                    first = half * BANK_TILES + part * PAIR_TILES
                    view = q_view[:, g * QPK + place : g * QPK + place + CHUNK_SLOTS, first : first + PAIR_TILES, :]

                    def dest(rows, view=view):
                        nc.sync.dma_start(out=view, in_=rows[:].rearrange("p (s j d) -> p s j d", s=CHUNK_SLOTS, d=HD))

                    if n in TENSOR_ADDS:
                        base = sums[ch, half][:, part * PAIR_TILES * HD : (part + 1) * PAIR_TILES * HD].unsqueeze(2).to_broadcast([P, PAIR_TILES * HD, 2])
                        waiting[n] = (((identity, base), (minus, pair[:])), CHUNK_SLOTS, dest)
                        continue
                    rows = work.tile([P, BANK], F32, tag="rows")
                    out, base, minuend = pair_views(rows, part, sums[ch, half], pair)
                    add(out=out, in0=base, in1=minuend, op=SUB)
                    dest(rows)
                elif kind == "value":
                    rows = work.tile([P, BANK], F32, tag="rows")
                    nc.scalar.copy(out=rows[:], in_=accs[n][:])
                    nc.sync.dma_start(out=v_view[:, g, tiles, :], in_=rows[:].rearrange("p (j d) -> p j d", d=HD))
                elif n == len(banks) - 1:
                    width = CHUNK_SLOTS * HD
                    halves = []
                    for j in range(PAIR_TILES):
                        both = work.tile([P, 2, BANK], F32, tag="both")
                        products(both, accs[n][:, j * width : (j + 1) * width], q_table[g], place, CHUNK_SLOTS, 1)
                        halves.append(both)
                    for j, combine in enumerate((G, V)):
                        rows = add_halves(combine, halves[j], CHUNK_SLOTS, 1)
                        first = half * BANK_TILES + part * PAIR_TILES + j
                        nc.sync.dma_start(
                            out=q_view[:, g * QPK + place : g * QPK + place + CHUNK_SLOTS, first : first + 1, :],
                            in_=rows[:, :width].rearrange("p (a j d) -> p a j d", a=CHUNK_SLOTS, d=HD),
                        )
                else:
                    both = work.tile([P, 2, BANK], F32, tag="both")
                    positions = 2
                    if kind == "key":
                        products(both, accs[n], k_table[g], half * positions, positions, 2)
                        view = k_view[:, g, tiles, :]

                        def dest(rows, view=view):
                            nc.sync.dma_start(out=view, in_=rows[:].rearrange("p (j d) -> p j d", d=HD))

                    else:
                        products(both, accs[n], q_table[g], place, positions, 2)
                        first = half * BANK_TILES + part * PAIR_TILES
                        view = q_view[:, g * QPK + place : g * QPK + place + CHUNK_SLOTS, first : first + PAIR_TILES, :]

                        def dest(rows, view=view):
                            nc.sync.dma_start(out=view, in_=rows[:].rearrange("p (a j d) -> p a j d", a=CHUNK_SLOTS, d=HD))

                    if n in TENSOR_ADDS:
                        waiting[n] = (((identity, both[:, 0, :]), (identity, both[:, 1, :])), positions, dest)
                        continue
                    dest(add_halves(add, both, positions, BANK_TILES // positions))
